import numpy as np
import ml_dtypes


def mxq(x, axis, fmt="e4m3"):
    dtype, down = {"e4m3": (ml_dtypes.float8_e4m3fn, 7), "e5m2": (ml_dtypes.float8_e5m2, 14)}[fmt]
    v = np.moveaxis(np.asarray(x, np.float32).astype(ml_dtypes.bfloat16).astype(np.float64), axis, -1)
    blocks = v.reshape(v.shape[:-1] + (-1, 32))
    amax = np.abs(blocks).max(-1, keepdims=True)
    byte = np.maximum(np.where(amax > 0, np.frexp(amax)[1] - 1 + 127, 0) - down, 1)
    scale = np.exp2(byte - 127.0)
    codes = (blocks / scale).astype(np.float32).astype(dtype).astype(np.float64)
    return np.moveaxis((codes * scale).reshape(v.shape), -1, axis)


WIDE = False


def mx_kscale(k):
    if not WIDE:
        return np.ones(k)
    levels = np.array([10, -10, 5, -5, 0])
    if k % 512:
        return np.exp2(np.random.permutation(np.resize(levels, k // 32))).repeat(32)
    a = np.empty((k // 512, 16))
    for p in range(k // 512):
        a[p, :8] = np.random.permutation(np.resize(levels, 8))
        for g in range(8):
            far = levels[np.abs(levels - a[p, g]) >= 10]
            a[p, g + 8] = far[np.random.randint(len(far))]
    return np.exp2(a.ravel()).repeat(32)


BF16 = ml_dtypes.bfloat16


def bf(x):
    return np.asarray(x, np.float32).astype(BF16)


def f64(x):
    return np.asarray(x).astype(np.float64)


B, S, D, F, N = 2, 1024, 1024, 1024, 1024
SPARSITY = 0.1


def make_theta_sign(d1, d2, gain, row, col):
    mask = np.random.random((d1, d2)) < SPARSITY
    mag = np.abs(np.random.standard_normal((d1, d2))) * gain / np.sqrt(SPARSITY * d1)
    th = np.where(mask, mag, -mag) / row[:, None] * col
    sign = np.where(np.random.random((d1, d2)) < 0.5, -1.0, 1.0)
    return bf(th), bf(sign)


def draw0():
    s, t = mx_kscale(D), mx_kscale(F)
    x = bf(np.random.standard_normal((B, S, D)) * s)
    th1, sign1 = make_theta_sign(D, F, 1.0, s, t)
    th2, sign2 = make_theta_sign(F, N, 1.4, t, np.ones(N))
    return {"x": x, "th1": th1, "sign1": sign1, "th2": th2, "sign2": sign2, "relu": 1}


def core(x, th1, sign1, th2, sign2, relu):
    x = f64(x)
    for th, sign in ((f64(th1), f64(sign1)), (f64(th2), f64(sign2))):
        w = th * sign * (th > 0)
        x = mxq(x, 2, "e4m3") @ mxq(w, 0, "e4m3")
        if relu:
            x = np.maximum(x, 0.0)
    return x


def e4m3fn_bytes(y):
    return np.clip(np.asarray(y, np.float64), -448.0, 448.0).astype(np.float32).astype(ml_dtypes.float8_e4m3fn).view(np.uint8)


def e4m3fn_values(b):
    return np.asarray(b, np.uint8).view(ml_dtypes.float8_e4m3fn).astype(np.float64)


def setup_inputs():
    d = draw0()
    x0 = np.asarray(d['x']).astype(np.float64)
    s = (np.max(np.abs(x0), axis=(0, 1), keepdims=True) / 448.0).astype(np.float32)
    out = {}
    for k, v in d.items():
        if k == 'x':
            out['x_bytes'] = e4m3fn_bytes(x0 / s.astype(np.float64))
            out['x_scale'] = s
        else:
            out[k] = v
    return out


def reference(x_bytes, x_scale, th1, sign1, th2, sign2, relu):
    return core(e4m3fn_values(x_bytes) * x_scale.astype(np.float64), th1, sign1, th2, sign2, relu)

@@ -1,0 +1,342 @@
+from contextlib import ExitStack
+
+import concourse.mybir as mybir
+from concourse.masks import make_identity
+
+TOKENS, D, F, N = 2048, 1024, 1024, 1024
+FLOPS = 2 * TOKENS * D * F + 2 * TOKENS * F * N
+
+F32 = mybir.dt.float32
+BF16 = mybir.dt.bfloat16
+U32 = mybir.dt.uint32
+U8 = mybir.dt.uint8
+FP8 = mybir.dt.float8_e4m3fn
+FP8X4 = mybir.dt.float8_e4m3fn_x4
+MAX = mybir.AluOpType.max
+MULT = mybir.AluOpType.mult
+RELU = mybir.ActivationFunctionType.Relu
+
+P = 128
+PACK = 4
+HALF = P * PACK
+
+LOADS = ((0, 2), (2, 2), (4, 4), (8, 4), (12, 4))
+GROUPS = ((0, 1), (1, 1), (2, 2), (4, 2), (6, 2), (8, 2), (10, 2), (12, 1), (13, 2), (15, 1))
+
+
+def tile_sparse_connect_kernel(tc, x_bytes, x_scale, th1, sign1, th2, sign2, relu, out):
+    assert relu == 1
+    nc = tc.nc
+    x_rows = x_bytes.flatten_outer_dims()
+    out_rows = out.flatten_outer_dims()
+    w1_hbm = [a.rearrange("(g p j) f -> g p j f", p=P, j=PACK) for a in (th1, sign1)]
+    w2_hbm = [a.rearrange("(g p j) f -> g p j f", p=P, j=PACK) for a in (th2, sign2)]
+    group_size = dict(GROUPS)
+
+    with ExitStack() as ctx:
+        keep = ctx.enter_context(tc.tile_pool(name="keep", bufs=1))
+        stage = ctx.enter_context(tc.tile_pool(name="stage", bufs=4))
+        work = ctx.enter_context(tc.tile_pool(name="work", bufs=6))
+        psum = ctx.enter_context(tc.psum_pool(name="psum", bufs=8))
+
+        identity = keep.tile([P, P], F32)
+        make_identity(nc, identity[:])
+        scale_column = keep.tile([P, 8], F32, align_bytes=64)
+        scale = keep.tile([P, D], F32, align_bytes=64)
+        x_codes_in = keep.tile([P, TOKENS // P, D], U8, align_bytes=64)
+
+        theta, sign, grouped, w_codes, w_scales = {}, {}, {}, {}, {}
+        x_tok, x_turned, x_grouped, x_codes, x_scales = {}, {}, {}, {}, {}
+        h_grouped, h_codes, h_scales = {}, {}, {}
+
+        def tiles_of(group):
+            return range(group, group + group_size[group])
+
+
+        def row_parts(layer, half, g):
+            return (slice(0, 2), slice(2, 4)) if (layer, half, g) == (1, 0, 0) else (slice(0, 4),)
+
+        def load_w1(half, g):
+            cols = slice(half * HALF, (half + 1) * HALF)
+            th = stage.tile([P, PACK, HALF], BF16, name="theta1", align_bytes=64)
+            sg = stage.tile([P, PACK, HALF], BF16, name="sign1", align_bytes=64)
+            for dst, src in ((th, w1_hbm[0][g]), (sg, w1_hbm[1][g])):
+                for rows in row_parts(1, half, g):
+                    nc.sync.dma_start(out=dst[:, rows], in_=src[:, rows, cols])
+            theta[1, half, g], sign[1, half, g] = th[:], sg[:]
+
+        def load_w2(g):
+            th = stage.tile([P, PACK, N], BF16, name="theta2", bufs=2, align_bytes=64)
+            nc.sync.dma_start(out=th[:], in_=w2_hbm[0][g])
+            sg = stage.tile([P, PACK, N], BF16, name="sign2", bufs=2, align_bytes=64)
+            nc.sync.dma_start(out=sg[:], in_=w2_hbm[1][g])
+            for half in (0, 1):
+                cols = slice(half * HALF, (half + 1) * HALF)
+                theta[2, half, g], sign[2, half, g] = th[:, :, cols], sg[:, :, cols]
+
+        def load_x(first, count):
+            nc.sync.dma_start(
+                out=x_codes_in[:, first : first + count],
+                in_=x_rows[first * P : (first + count) * P, :].rearrange("(p c) d -> p c d", c=count),
+            )
+
+        def spread_scale():
+            for b in (0, 1):
+                bank = psum.tile([P, PACK, P], F32, name="scale_bank", tag="bank")
+                for c in range(PACK):
+                    column = scale_column[:, PACK * b + c : PACK * b + c + 1]
+                    nc.tensor.matmul(
+                        out=bank[:, c], lhsT=column.to_broadcast([P, P]), rhs=identity[:], start=True, stop=True
+                    )
+                nc.scalar.copy(
+                    out=scale[:].rearrange("p (q c) -> p q c", c=8)[:, :, PACK * b : PACK * (b + 1)],
+                    in_=bank[:].rearrange("p c q -> p q c"),
+                )
+
+
+        def relu_w(layer, half, g):
+            th = theta[layer, half, g]
+            for rows in row_parts(layer, half, g):
+                nc.vector.tensor_scalar(out=th[:, rows], in0=th[:, rows], scalar1=0.0, scalar2=None, op0=MAX)
+
+        def sign_w(layer, half, g):
+            th, sg = theta[layer, half, g], sign[layer, half, g]
+            for rows in row_parts(layer, half, g):
+                nc.vector.tensor_tensor(out=th[:, rows], in0=th[:, rows], in1=sg[:, rows], op=MULT)
+
+        def interleave_w(layer, half, g, copy):
+            w = stage.tile([P, HALF * PACK], BF16, name="w_grouped", bufs=3, align_bytes=64)
+            th = theta[layer, half, g]
+            if layer == 1:
+                copy(
+                    out=w[:].rearrange("p (t m j) -> p m t j", t=PACK, j=PACK),
+                    in_=th.rearrange("p j (m t) -> p m t j", t=PACK),
+                )
+            else:
+                copy(
+                    out=w[:].rearrange("p (c i j) -> p c j i", i=4, j=PACK),
+                    in_=th.rearrange("p j (c i) -> p c j i", i=4),
+                )
+            grouped[layer, half, g] = w
+
+        def quantize_w(layer, half, g):
+            codes = keep.tile([P, HALF], U32, name=f"w_codes{layer}{half}{g}", align_bytes=64)
+            scales = keep.tile([P, HALF], U8, name=f"w_scales{layer}{half}{g}", align_bytes=64)
+            nc.vector.quantize_mx(out=codes[:].bitcast(FP8X4), scales=scales[:], in_=grouped[layer, half, g][:])
+            w_codes[layer, half, g], w_scales[layer, half, g] = codes, scales
+
+
+        def multiply_x(i):
+            t = work.tile([P, D], BF16, name="x_tok", align_bytes=64)
+            nc.vector.tensor_tensor(out=t[:], in0=x_codes_in[:, i].bitcast(FP8), in1=scale[:], op=MULT)
+            x_tok[i] = t
+
+        def turn_x(i):
+            words = x_tok[i][:].bitcast(F32)
+            bank = psum.tile([P, 2, 2, P], F32, name="x_bank", tag="bank")
+            for g in (0, 1):
+                for u in (0, 1):
+                    nc.tensor.transpose(bank[:, g, u], words[:, 256 * g + u : 256 * (g + 1) : 2], identity[:])
+            group = max(first for first, _ in GROUPS if first <= i)
+            if i == group:
+                x_grouped[group] = work.tile([P, group_size[group], 2, P, 2], F32, name="x_grouped", bufs=4, align_bytes=64)
+            nc.scalar.copy(out=x_grouped[group][:, i - group], in_=bank[:].rearrange("p g u r -> p g r u"))
+
+        def quantize_x(group):
+            count = group_size[group]
+            codes = work.tile([P, count, 2, P], U32, name="x_codes", bufs=6, align_bytes=64)
+            scales = work.tile([P, count, 2, P], U8, name="x_scales", bufs=6, align_bytes=64)
+            nc.vector.quantize_mx(
+                out=codes[:].rearrange("p c g r -> p (c g r)").bitcast(FP8X4),
+                scales=scales[:].rearrange("p c g r -> p (c g r)"),
+                in_=x_grouped[group][:].rearrange("p c g r u -> p (c g r u)").bitcast(BF16),
+            )
+            for c, i in enumerate(tiles_of(group)):
+                x_codes[i], x_scales[i] = codes[:, c], scales[:, c]
+
+
+        def layer1(group, half):
+            if half == 0:
+                h_grouped[group] = work.tile(
+                    [P, group_size[group], 2, P, PACK], BF16, name="h_grouped", bufs=7, align_bytes=64
+                )
+            for c, i in enumerate(tiles_of(group)):
+                bank = psum.tile([P, PACK, P], F32, name="h_bank", tag="bank")
+                for t in range(PACK):
+                    cols = slice(t * P, (t + 1) * P)
+                    for g in (0, 1):
+                        nc.tensor.matmul_mx(
+                            out=bank[:, t],
+                            lhsT=w_codes[1, half, g][:, cols].bitcast(FP8X4),
+                            lhsT_scale=w_scales[1, half, g][:, cols],
+                            rhs=x_codes[i][:, g].bitcast(FP8X4),
+                            rhs_scale=x_scales[i][:, g],
+                            start=(g == 0),
+                            stop=(g == 1),
+                        )
+                nc.scalar.activation(
+                    out=h_grouped[group][:, c, half], in_=bank[:].rearrange("p t n -> p n t"), func=RELU
+                )
+
+        def quantize_h(group):
+            count = group_size[group]
+            codes = work.tile([P, count, 2, P], U32, name="h_codes", bufs=len(GROUPS), align_bytes=64)
+            scales = work.tile([P, count, 2, P], U8, name="h_scales", bufs=len(GROUPS), align_bytes=64)
+            nc.vector.quantize_mx(
+                out=codes[:].rearrange("p c g n -> p (c g n)").bitcast(FP8X4),
+                scales=scales[:].rearrange("p c g n -> p (c g n)"),
+                in_=h_grouped[group][:].rearrange("p c g n t -> p (c g n t)"),
+            )
+            for c, i in enumerate(tiles_of(group)):
+                h_codes[i], h_scales[i] = codes[:, c], scales[:, c]
+
+
+        def layer2(group, half, vector_tiles=()):
+            cols = slice(half * HALF, (half + 1) * HALF)
+            for i in tiles_of(group):
+                bank = psum.tile([P, HALF], F32, name="out_bank", tag="bank")
+                for g in (0, 1):
+                    nc.tensor.matmul_mx(
+                        out=bank[:],
+                        lhsT=h_codes[i][:, g].bitcast(FP8X4),
+                        lhsT_scale=h_scales[i][:, g],
+                        rhs=w_codes[2, half, g][:].bitcast(FP8X4),
+                        rhs_scale=w_scales[2, half, g][:],
+                        start=(g == 0),
+                        stop=(g == 1),
+                    )
+                result = work.tile([P, HALF], F32, name="result", bufs=8, align_bytes=64)
+                if i in vector_tiles:
+                    nc.vector.tensor_scalar(out=result[:], in0=bank[:], scalar1=0.0, scalar2=None, op0=MAX)
+                else:
+                    nc.scalar.activation(out=result[:], in_=bank[:], func=RELU)
+                first, count = max(load for load in LOADS if load[0] <= i)
+                rows = out_rows[first * P : (first + count) * P, :].rearrange("(p c) n -> c p n", c=count)
+                nc.sync.dma_start(out=rows[i - first][:, cols], in_=result[:])
+
+
+        scalar_copy, vector_copy = nc.scalar.copy, nc.vector.tensor_copy
+
+        with tc.manual_schedule():
+            nc.scalar.dma_start(out=scale_column[:], in_=x_scale.rearrange("a b (p c) -> p (a b c)", c=8))
+            load_w1(0, 0)
+            load_x(*LOADS[0])
+            load_w1(0, 1)
+            load_x(*LOADS[1])
+            load_w1(1, 0)
+            load_w1(1, 1)
+            load_x(*LOADS[2])
+            load_w2(0)
+            load_w2(1)
+            load_x(*LOADS[3])
+            load_x(*LOADS[4])
+            spread_scale()
+
+            relu_w(1, 0, 0)
+            sign_w(1, 0, 0)
+            interleave_w(1, 0, 0, scalar_copy)
+            relu_w(1, 0, 1)
+            multiply_x(0)
+            turn_x(0)
+            sign_w(1, 0, 1)
+            interleave_w(1, 0, 1, scalar_copy)
+            multiply_x(1)
+            turn_x(1)
+            relu_w(1, 1, 0)
+            multiply_x(2)
+            turn_x(2)
+            quantize_x(0)
+            sign_w(1, 1, 0)
+            interleave_w(1, 1, 0, scalar_copy)
+            relu_w(1, 1, 1)
+            multiply_x(3)
+            sign_w(1, 1, 1)
+            interleave_w(1, 1, 1, scalar_copy)
+            turn_x(3)
+            multiply_x(4)
+            turn_x(4)
+            quantize_w(1, 0, 0)
+            quantize_w(1, 0, 1)
+            multiply_x(5)
+            turn_x(5)
+            layer1(0, 0)
+            for i in (6, 7):
+                multiply_x(i)
+                turn_x(i)
+            quantize_x(1)
+            quantize_x(2)
+            quantize_w(1, 1, 0)
+            quantize_w(1, 1, 1)
+
+            layer1(1, 0)
+            layer1(2, 0)
+            relu_w(2, 0, 0)
+            quantize_x(4)
+            layer1(0, 1)
+            layer1(1, 1)
+            sign_w(2, 0, 0)
+            interleave_w(2, 0, 0, scalar_copy)
+            layer1(2, 1)
+            quantize_x(6)
+            layer1(4, 0)
+            layer1(4, 1)
+            for i in range(8, 12):
+                multiply_x(i)
+                turn_x(i)
+            layer1(6, 0)
+            layer1(6, 1)
+            for i in range(12, 16):
+                multiply_x(i)
+                turn_x(i)
+            quantize_x(8)
+            relu_w(2, 0, 1)
+            quantize_h(0)
+            quantize_h(1)
+            layer1(8, 0)
+            layer1(8, 1)
+            quantize_x(10)
+            sign_w(2, 0, 1)
+            quantize_h(2)
+            interleave_w(2, 0, 1, vector_copy)
+            layer1(10, 0)
+            layer1(10, 1)
+            quantize_x(12)
+            quantize_w(2, 0, 0)
+            quantize_w(2, 0, 1)
+            layer1(12, 0)
+            layer1(12, 1)
+
+            quantize_h(4)
+            quantize_h(6)
+            for group in (0, 1, 2, 4):
+                layer2(group, 0)
+            relu_w(2, 1, 0)
+            quantize_x(13)
+            quantize_x(15)
+            layer1(13, 0)
+            layer1(13, 1)
+            quantize_h(8)
+            quantize_h(10)
+            sign_w(2, 1, 0)
+            relu_w(2, 1, 1)
+            quantize_h(12)
+            sign_w(2, 1, 1)
+            interleave_w(2, 1, 0, vector_copy)
+            interleave_w(2, 1, 1, vector_copy)
+            for group in (6, 8, 10, 12):
+                layer2(group, 0)
+            quantize_h(13)
+            layer2(13, 0)
+
+            quantize_w(2, 1, 0)
+            quantize_w(2, 1, 1)
+            odd_tiles = range(1, 12, 2)
+            for group in (0, 1, 2, 4, 6, 8, 10):
+                layer2(group, 1, odd_tiles)
+            layer1(15, 0)
+            layer1(15, 1)
+            quantize_h(15)
+            for group in (12, 13):
+                layer2(group, 1)
+            layer2(15, 0)
+            layer2(15, 1)

@@ -19,9 +19,10 @@ RELU = mybir.ActivationFunctionType.Relu
 P = 128
 PACK = 4
 HALF = P * PACK
+BANKS = 8
 
-LOADS = ((0, 2), (2, 2), (4, 4), (8, 4), (12, 4))
-GROUPS = ((0, 1), (1, 1), (2, 2), (4, 2), (6, 2), (8, 2), (10, 2), (12, 1), (13, 2), (15, 1))
+LOADS = ((0, 2), (2, 2), (4, 2), (6, 2), (8, 4), (12, 4))
+GROUPS = ((0, 2), (2, 2), (4, 2), (6, 2), (8, 2), (10, 2), (12, 2), (14, 1), (15, 1))
 
 
 def tile_sparse_connect_kernel(tc, x_bytes, x_scale, th1, sign1, th2, sign2, relu, out):
@@ -29,159 +30,209 @@ def tile_sparse_connect_kernel(tc, x_bytes, x_scale, th1, sign1, th2, sign2, rel
     nc = tc.nc
     x_rows = x_bytes.flatten_outer_dims()
     out_rows = out.flatten_outer_dims()
-    w1_hbm = [a.rearrange("(g p j) f -> g p j f", p=P, j=PACK) for a in (th1, sign1)]
-    w2_hbm = [a.rearrange("(g p j) f -> g p j f", p=P, j=PACK) for a in (th2, sign2)]
+    theta_hbm = {n: a.rearrange("(g p j) f -> g p j f", p=P, j=PACK) for n, a in ((1, th1), (2, th2))}
+    sign_hbm = {n: a.rearrange("(g p j) f -> g p j f", p=P, j=PACK) for n, a in ((1, sign1), (2, sign2))}
     group_size = dict(GROUPS)
 
     with ExitStack() as ctx:
         keep = ctx.enter_context(tc.tile_pool(name="keep", bufs=1))
-        stage = ctx.enter_context(tc.tile_pool(name="stage", bufs=4))
-        work = ctx.enter_context(tc.tile_pool(name="work", bufs=6))
-        psum = ctx.enter_context(tc.psum_pool(name="psum", bufs=8))
+        work = ctx.enter_context(tc.tile_pool(name="work", bufs=1))
+        psum = ctx.enter_context(tc.psum_pool(name="psum", bufs=1))
 
-        identity = keep.tile([P, P], F32)
+        identity = keep.tile([P, P], F32, name="identity")
         make_identity(nc, identity[:])
-        scale_column = keep.tile([P, 8], F32, align_bytes=64)
-        scale = keep.tile([P, D], F32, align_bytes=64)
-        x_codes_in = keep.tile([P, TOKENS // P, D], U8, align_bytes=64)
+        identity_bf16 = keep.tile([P, P], BF16, name="identity_bf16")
+        make_identity(nc, identity_bf16[:])
+        scale = keep.tile([P, 2, PACK], F32, name="scale", align_bytes=64)
 
-        theta, sign, grouped, w_codes, w_scales = {}, {}, {}, {}, {}
-        x_tok, x_turned, x_grouped, x_codes, x_scales = {}, {}, {}, {}, {}
-        h_grouped, h_codes, h_scales = {}, {}, {}
+        theta, sign, masked, sign_banks, grouped, w_codes, w_scales = {}, {}, {}, {}, {}, {}, {}
+        x_in, x_wide, x_banks, x_grouped, x_codes, x_scales = {}, {}, {}, {}, {}, {}
+        h_banks, h_grouped, h_codes, h_scales = {}, {}, {}, {}
+        free_banks = list(range(BANKS))
+
+        def take_bank(shape, dtype, name):
+            number = free_banks[0]
+            free_banks.remove(number)
+            return psum.tile(shape, dtype, name=name, tag=f"bank{number}"), number
 
         def tiles_of(group):
             return range(group, group + group_size[group])
 
+        def group_of(i):
+            return max(first for first, count in GROUPS if first <= i)
 
-        def row_parts(layer, half, g):
-            return (slice(0, 2), slice(2, 4)) if (layer, half, g) == (1, 0, 0) else (slice(0, 4),)
+        def relu_out_of_psum(out, in_, on_vector):
+            if on_vector:
+                nc.vector.tensor_scalar(out=out, in0=in_, scalar1=0.0, scalar2=None, op0=MAX)
+            else:
+                nc.scalar.activation(out=out, in_=in_, func=RELU)
 
-        def load_w1(half, g):
-            cols = slice(half * HALF, (half + 1) * HALF)
-            th = stage.tile([P, PACK, HALF], BF16, name="theta1", align_bytes=64)
-            sg = stage.tile([P, PACK, HALF], BF16, name="sign1", align_bytes=64)
-            for dst, src in ((th, w1_hbm[0][g]), (sg, w1_hbm[1][g])):
-                for rows in row_parts(1, half, g):
-                    nc.sync.dma_start(out=dst[:, rows], in_=src[:, rows, cols])
-            theta[1, half, g], sign[1, half, g] = th[:], sg[:]
 
-        def load_w2(g):
-            th = stage.tile([P, PACK, N], BF16, name="theta2", bufs=2, align_bytes=64)
-            nc.sync.dma_start(out=th[:], in_=w2_hbm[0][g])
-            sg = stage.tile([P, PACK, N], BF16, name="sign2", bufs=2, align_bytes=64)
-            nc.sync.dma_start(out=sg[:], in_=w2_hbm[1][g])
+        def load_w1(hbm, pieces, half, g):
+            t = keep.tile([P, PACK, HALF], BF16, name=f"w1_in{len(theta) + len(sign)}", align_bytes=64)
+            nc.sync.dma_start(out=t[:], in_=hbm[1][g][:, :, half * HALF : (half + 1) * HALF])
+            pieces[1, half, g] = t[:]
+
+        def load_w2(hbm, pieces, g):
+            t = keep.tile([P, PACK, N], BF16, name=f"w2_in{len(theta) + len(sign)}", align_bytes=64)
+            nc.sync.dma_start(out=t[:], in_=hbm[2][g])
             for half in (0, 1):
-                cols = slice(half * HALF, (half + 1) * HALF)
-                theta[2, half, g], sign[2, half, g] = th[:, :, cols], sg[:, :, cols]
+                pieces[2, half, g] = t[:, :, half * HALF : (half + 1) * HALF]
 
         def load_x(first, count):
+            t = keep.tile([P, count, D], U8, name=f"x_bytes{first}", align_bytes=64)
             nc.sync.dma_start(
-                out=x_codes_in[:, first : first + count],
-                in_=x_rows[first * P : (first + count) * P, :].rearrange("(p c) d -> p c d", c=count),
+                out=t[:], in_=x_rows[first * P : (first + count) * P, :].rearrange("(p c) d -> p c d", c=count)
+            )
+            for c in range(count):
+                x_in[first + c] = t[:, c]
+
+
+        def grouped_tile(piece):
+            grouped[piece] = work.tile([P, HALF * PACK], BF16, name="w_grouped", bufs=3, align_bytes=64)
+            return grouped[piece]
+
+        def relu_interleave_theta(*piece):
+            t = work.tile([P, HALF, PACK], BF16, name="w_masked", bufs=2, align_bytes=64)
+            nc.scalar.activation(
+                out=t[:].rearrange("p (c i) j -> p c j i", i=4),
+                in_=theta[piece].rearrange("p j (c i) -> p c j i", i=4),
+                func=RELU,
+            )
+            masked[piece] = t
+
+        def interleave_sign(*piece):
+            sign_banks[piece] = []
+            for b in (0, 1):
+                bank, number = take_bank([P, 2, P, PACK], BF16, "sign_bank")
+                for q in (0, 1):
+                    cols = slice((2 * b + q) * P, (2 * b + q + 1) * P)
+                    nc.tensor.matmul(
+                        out=bank[:, q].rearrange("p c j -> p (c j)"),
+                        lhsT=identity_bf16[:],
+                        rhs=sign[piece][:, :, cols].rearrange("p j c -> p c j"),
+                        start=True,
+                        stop=True,
+                    )
+                sign_banks[piece].append((bank, number))
+
+        def multiply_w1(*piece):
+            w = grouped_tile(piece)
+            for b, (bank, number) in enumerate(sign_banks[piece]):
+                nc.vector.tensor_tensor(
+                    out=w[:].rearrange("p (t m j) -> p t m j", t=PACK, j=PACK)[:, :, b * 64 : (b + 1) * 64],
+                    in0=bank[:].rearrange("p q (m t) j -> p t (q m) j", t=PACK),
+                    in1=masked[piece][:, b * 256 : (b + 1) * 256].rearrange("p (m t) j -> p t m j", t=PACK),
+                    op=MULT,
+                )
+                free_banks.append(number)
+
+        def relu_w2(*piece):
+            th = theta[piece]
+            nc.vector.tensor_scalar(out=th, in0=th, scalar1=0.0, scalar2=None, op0=MAX)
+
+        def multiply_w2(*piece):
+            th = theta[piece]
+            nc.vector.tensor_tensor(out=th, in0=th, in1=sign[piece], op=MULT)
+
+        def interleave_w2(piece, copy):
+            copy(
+                out=grouped_tile(piece)[:].rearrange("p (c i j) -> p c j i", i=4, j=PACK),
+                in_=theta[piece].rearrange("p j (c i) -> p c j i", i=4),
             )
 
-        def spread_scale():
-            for b in (0, 1):
-                bank = psum.tile([P, PACK, P], F32, name="scale_bank", tag="bank")
-                for c in range(PACK):
-                    column = scale_column[:, PACK * b + c : PACK * b + c + 1]
-                    nc.tensor.matmul(
-                        out=bank[:, c], lhsT=column.to_broadcast([P, P]), rhs=identity[:], start=True, stop=True
-                    )
-                nc.scalar.copy(
-                    out=scale[:].rearrange("p (q c) -> p q c", c=8)[:, :, PACK * b : PACK * (b + 1)],
-                    in_=bank[:].rearrange("p c q -> p q c"),
-                )
-
-
-        def relu_w(layer, half, g):
-            th = theta[layer, half, g]
-            for rows in row_parts(layer, half, g):
-                nc.vector.tensor_scalar(out=th[:, rows], in0=th[:, rows], scalar1=0.0, scalar2=None, op0=MAX)
-
-        def sign_w(layer, half, g):
-            th, sg = theta[layer, half, g], sign[layer, half, g]
-            for rows in row_parts(layer, half, g):
-                nc.vector.tensor_tensor(out=th[:, rows], in0=th[:, rows], in1=sg[:, rows], op=MULT)
-
-        def interleave_w(layer, half, g, copy):
-            w = stage.tile([P, HALF * PACK], BF16, name="w_grouped", bufs=3, align_bytes=64)
-            th = theta[layer, half, g]
-            if layer == 1:
-                copy(
-                    out=w[:].rearrange("p (t m j) -> p m t j", t=PACK, j=PACK),
-                    in_=th.rearrange("p j (m t) -> p m t j", t=PACK),
-                )
-            else:
-                copy(
-                    out=w[:].rearrange("p (c i j) -> p c j i", i=4, j=PACK),
-                    in_=th.rearrange("p j (c i) -> p c j i", i=4),
-                )
-            grouped[layer, half, g] = w
-
-        def quantize_w(layer, half, g):
+        def quantize_w(*piece):
+            layer, half, g = piece
             codes = keep.tile([P, HALF], U32, name=f"w_codes{layer}{half}{g}", align_bytes=64)
             scales = keep.tile([P, HALF], U8, name=f"w_scales{layer}{half}{g}", align_bytes=64)
-            nc.vector.quantize_mx(out=codes[:].bitcast(FP8X4), scales=scales[:], in_=grouped[layer, half, g][:])
-            w_codes[layer, half, g], w_scales[layer, half, g] = codes, scales
+            nc.vector.quantize_mx(out=codes[:].bitcast(FP8X4), scales=scales[:], in_=grouped[piece][:])
+            w_codes[piece], w_scales[piece] = codes, scales
 
 
-        def multiply_x(i):
-            t = work.tile([P, D], BF16, name="x_tok", align_bytes=64)
-            nc.vector.tensor_tensor(out=t[:], in0=x_codes_in[:, i].bitcast(FP8), in1=scale[:], op=MULT)
-            x_tok[i] = t
+        def widen_x(tiles, copy):
+            for i in tiles:
+                x_wide[i] = work.tile([P, D], BF16, name="x_wide", bufs=6, align_bytes=64)
+                copy(out=x_wide[i][:], in_=x_in[i].bitcast(FP8))
 
-        def turn_x(i):
-            words = x_tok[i][:].bitcast(F32)
-            bank = psum.tile([P, 2, 2, P], F32, name="x_bank", tag="bank")
-            for g in (0, 1):
-                for u in (0, 1):
-                    nc.tensor.transpose(bank[:, g, u], words[:, 256 * g + u : 256 * (g + 1) : 2], identity[:])
-            group = max(first for first, _ in GROUPS if first <= i)
-            if i == group:
-                x_grouped[group] = work.tile([P, group_size[group], 2, P, 2], F32, name="x_grouped", bufs=4, align_bytes=64)
-            nc.scalar.copy(out=x_grouped[group][:, i - group], in_=bank[:].rearrange("p g u r -> p g r u"))
+        def turn_x(*tiles):
+            for i in tiles:
+                words = x_wide[i][:].bitcast(F32)
+                bank, number = take_bank([P, 2, 2, P], F32, "x_bank")
+                for g in (0, 1):
+                    for u in (0, 1):
+                        nc.tensor.transpose(bank[:, u, g], words[:, 256 * g + u : 256 * (g + 1) : 2], identity[:])
+                x_banks[i] = bank, number
+
+        def scale_x(*tiles):
+            for i in tiles:
+                group = group_of(i)
+                if i == group:
+                    x_grouped[group] = work.tile([P, group_size[group], D], BF16, name="x_grouped", bufs=3, align_bytes=64)
+                bank, number = x_banks[i]
+                values = bank[:].rearrange("p u g r -> p (u g r)").bitcast(BF16)
+                nc.vector.tensor_tensor(
+                    out=x_grouped[group][:, i - group].rearrange("p (g r u e) -> p g r u e", g=2, u=2, e=2),
+                    in0=values.rearrange("p (u g r e) -> p g r u e", u=2, g=2, e=2),
+                    in1=scale[:].rearrange("p g (u e) -> p g u e", u=2).unsqueeze(2).to_broadcast([P, 2, P, 2, 2]),
+                    op=MULT,
+                )
+                free_banks.append(number)
 
         def quantize_x(group):
             count = group_size[group]
-            codes = work.tile([P, count, 2, P], U32, name="x_codes", bufs=6, align_bytes=64)
-            scales = work.tile([P, count, 2, P], U8, name="x_scales", bufs=6, align_bytes=64)
+            codes = work.tile([P, count, 2, P], U32, name="x_codes", bufs=5, align_bytes=64)
+            scales = work.tile([P, count, 2, P], U8, name="x_scales", bufs=5, align_bytes=64)
             nc.vector.quantize_mx(
                 out=codes[:].rearrange("p c g r -> p (c g r)").bitcast(FP8X4),
                 scales=scales[:].rearrange("p c g r -> p (c g r)"),
-                in_=x_grouped[group][:].rearrange("p c g r u -> p (c g r u)").bitcast(BF16),
+                in_=x_grouped[group][:].rearrange("p c d -> p (c d)"),
             )
             for c, i in enumerate(tiles_of(group)):
                 x_codes[i], x_scales[i] = codes[:, c], scales[:, c]
 
 
-        def layer1(group, half):
-            if half == 0:
-                h_grouped[group] = work.tile(
-                    [P, group_size[group], 2, P, PACK], BF16, name="h_grouped", bufs=7, align_bytes=64
-                )
-            for c, i in enumerate(tiles_of(group)):
-                bank = psum.tile([P, PACK, P], F32, name="h_bank", tag="bank")
-                for t in range(PACK):
-                    cols = slice(t * P, (t + 1) * P)
-                    for g in (0, 1):
-                        nc.tensor.matmul_mx(
-                            out=bank[:, t],
-                            lhsT=w_codes[1, half, g][:, cols].bitcast(FP8X4),
-                            lhsT_scale=w_scales[1, half, g][:, cols],
-                            rhs=x_codes[i][:, g].bitcast(FP8X4),
-                            rhs_scale=x_scales[i][:, g],
-                            start=(g == 0),
-                            stop=(g == 1),
-                        )
-                nc.scalar.activation(
-                    out=h_grouped[group][:, c, half], in_=bank[:].rearrange("p t n -> p n t"), func=RELU
-                )
+        def multiply_layer1(tiles, halves):
+            for i in tiles:
+                for half in halves:
+                    bank, number = take_bank([P, PACK, P], F32, "h_bank")
+                    for t in range(PACK):
+                        cols = slice(t * P, (t + 1) * P)
+                        for g in (0, 1):
+                            nc.tensor.matmul_mx(
+                                out=bank[:, t],
+                                lhsT=w_codes[1, half, g][:, cols].bitcast(FP8X4),
+                                lhsT_scale=w_scales[1, half, g][:, cols],
+                                rhs=x_codes[i][:, g].bitcast(FP8X4),
+                                rhs_scale=x_scales[i][:, g],
+                                start=(g == 0),
+                                stop=(g == 1),
+                            )
+                    h_banks[i, half] = bank, number
+
+        def empty_layer1(tiles, halves):
+            for i in tiles:
+                group = group_of(i)
+                if group not in h_grouped:
+                    h_grouped[group] = work.tile(
+                        [P, group_size[group], 2, P, PACK], BF16, name="h_grouped", bufs=7, align_bytes=64
+                    )
+                for half in halves:
+                    bank, number = h_banks[i, half]
+                    nc.scalar.activation(
+                        out=h_grouped[group][:, i - group, half], in_=bank[:].rearrange("p t n -> p n t"), func=RELU
+                    )
+                    free_banks.append(number)
+
+        def layer1(tiles, halves=(0, 1)):
+            for i in tiles:
+                for half in halves:
+                    multiply_layer1((i,), (half,))
+                    empty_layer1((i,), (half,))
 
         def quantize_h(group):
             count = group_size[group]
-            codes = work.tile([P, count, 2, P], U32, name="h_codes", bufs=len(GROUPS), align_bytes=64)
-            scales = work.tile([P, count, 2, P], U8, name="h_scales", bufs=len(GROUPS), align_bytes=64)
+            codes = keep.tile([P, count, 2, P], U32, name=f"h_codes{group}", align_bytes=64)
+            scales = keep.tile([P, count, 2, P], U8, name=f"h_scales{group}", align_bytes=64)
             nc.vector.quantize_mx(
                 out=codes[:].rearrange("p c g n -> p (c g n)").bitcast(FP8X4),
                 scales=scales[:].rearrange("p c g n -> p (c g n)"),
@@ -191,152 +242,154 @@ def tile_sparse_connect_kernel(tc, x_bytes, x_scale, th1, sign1, th2, sign2, rel
                 h_codes[i], h_scales[i] = codes[:, c], scales[:, c]
 
 
-        def layer2(group, half, vector_tiles=()):
-            cols = slice(half * HALF, (half + 1) * HALF)
-            for i in tiles_of(group):
-                bank = psum.tile([P, HALF], F32, name="out_bank", tag="bank")
-                for g in (0, 1):
-                    nc.tensor.matmul_mx(
-                        out=bank[:],
-                        lhsT=h_codes[i][:, g].bitcast(FP8X4),
-                        lhsT_scale=h_scales[i][:, g],
-                        rhs=w_codes[2, half, g][:].bitcast(FP8X4),
-                        rhs_scale=w_scales[2, half, g][:],
-                        start=(g == 0),
-                        stop=(g == 1),
-                    )
-                result = work.tile([P, HALF], F32, name="result", bufs=8, align_bytes=64)
-                if i in vector_tiles:
-                    nc.vector.tensor_scalar(out=result[:], in0=bank[:], scalar1=0.0, scalar2=None, op0=MAX)
-                else:
-                    nc.scalar.activation(out=result[:], in_=bank[:], func=RELU)
-                first, count = max(load for load in LOADS if load[0] <= i)
-                rows = out_rows[first * P : (first + count) * P, :].rearrange("(p c) n -> c p n", c=count)
-                nc.sync.dma_start(out=rows[i - first][:, cols], in_=result[:])
+        def layer2(tiles, halves, on_vector=()):
+            for i in tiles:
+                for half in halves:
+                    bank, number = take_bank([P, HALF], F32, "out_bank")
+                    for g in (0, 1):
+                        nc.tensor.matmul_mx(
+                            out=bank[:],
+                            lhsT=h_codes[i][:, g].bitcast(FP8X4),
+                            lhsT_scale=h_scales[i][:, g],
+                            rhs=w_codes[2, half, g][:].bitcast(FP8X4),
+                            rhs_scale=w_scales[2, half, g][:],
+                            start=(g == 0),
+                            stop=(g == 1),
+                        )
+                    result = work.tile([P, HALF], F32, name="result", bufs=8, align_bytes=64)
+                    relu_out_of_psum(result[:], bank[:], (i, half) in on_vector)
+                    free_banks.append(number)
+                    first, count = max(load for load in LOADS if load[0] <= i)
+                    rows = out_rows[first * P : (first + count) * P, :].rearrange("(p c) n -> c p n", c=count)
+                    nc.sync.dma_start(out=rows[i - first][:, half * HALF : (half + 1) * HALF], in_=result[:])
 
 
         scalar_copy, vector_copy = nc.scalar.copy, nc.vector.tensor_copy
 
         with tc.manual_schedule():
-            nc.scalar.dma_start(out=scale_column[:], in_=x_scale.rearrange("a b (p c) -> p (a b c)", c=8))
-            load_w1(0, 0)
-            load_x(*LOADS[0])
-            load_w1(0, 1)
-            load_x(*LOADS[1])
-            load_w1(1, 0)
-            load_w1(1, 1)
-            load_x(*LOADS[2])
-            load_w2(0)
-            load_w2(1)
+            nc.scalar.dma_start(out=scale[:], in_=x_scale.rearrange("a b (g p t) -> p (a b g) t", g=2, t=PACK))
+            for half in (0, 1):
+                for g in (0, 1):
+                    load_w1(theta_hbm, theta, half, g)
+                    if (half, g) == (0, 0):
+                        load_x(*LOADS[0])
+                    if (half, g) == (0, 1):
+                        load_x(*LOADS[1])
+                    load_w1(sign_hbm, sign, half, g)
+                    if (half, g) == (1, 0):
+                        load_x(*LOADS[2])
             load_x(*LOADS[3])
             load_x(*LOADS[4])
-            spread_scale()
+            for g in (0, 1):
+                load_w2(theta_hbm, theta, g)
+                load_w2(sign_hbm, sign, g)
+            load_x(*LOADS[5])
 
-            relu_w(1, 0, 0)
-            sign_w(1, 0, 0)
-            interleave_w(1, 0, 0, scalar_copy)
-            relu_w(1, 0, 1)
-            multiply_x(0)
-            turn_x(0)
-            sign_w(1, 0, 1)
-            interleave_w(1, 0, 1, scalar_copy)
-            multiply_x(1)
-            turn_x(1)
-            relu_w(1, 1, 0)
-            multiply_x(2)
-            turn_x(2)
+            widen_x((0, 1), vector_copy)
+            relu_interleave_theta(1, 0, 0)
+            turn_x(0, 1)
+            interleave_sign(1, 0, 0)
+            scale_x(0, 1)
+            relu_interleave_theta(1, 0, 1)
+            multiply_w1(1, 0, 0)
             quantize_x(0)
-            sign_w(1, 1, 0)
-            interleave_w(1, 1, 0, scalar_copy)
-            relu_w(1, 1, 1)
-            multiply_x(3)
-            sign_w(1, 1, 1)
-            interleave_w(1, 1, 1, scalar_copy)
-            turn_x(3)
-            multiply_x(4)
-            turn_x(4)
+            interleave_sign(1, 0, 1)
             quantize_w(1, 0, 0)
+            widen_x((2, 3), scalar_copy)
+            turn_x(2, 3)
+            multiply_w1(1, 0, 1)
+            scale_x(2)
             quantize_w(1, 0, 1)
-            multiply_x(5)
-            turn_x(5)
-            layer1(0, 0)
-            for i in (6, 7):
-                multiply_x(i)
-                turn_x(i)
-            quantize_x(1)
+            relu_interleave_theta(1, 1, 0)
+            interleave_sign(1, 1, 0)
+            scale_x(3)
+            widen_x((4, 5), scalar_copy)
+            relu_interleave_theta(1, 1, 1)
+            widen_x((6, 7, 8, 9), scalar_copy)
+            multiply_layer1((0,), (0,))
+            multiply_w1(1, 1, 0)
             quantize_x(2)
+            turn_x(4, 5)
+            multiply_layer1((1,), (0,))
+            scale_x(4)
             quantize_w(1, 1, 0)
+            interleave_sign(1, 1, 1)
+            multiply_w1(1, 1, 1)
+            multiply_layer1((2, 3), (0,))
+            scale_x(5)
             quantize_w(1, 1, 1)
-
-            layer1(1, 0)
-            layer1(2, 0)
-            relu_w(2, 0, 0)
             quantize_x(4)
-            layer1(0, 1)
-            layer1(1, 1)
-            sign_w(2, 0, 0)
-            interleave_w(2, 0, 0, scalar_copy)
-            layer1(2, 1)
+            turn_x(6, 7)
+            empty_layer1(range(4), (0,))
+
+            relu_w2(2, 0, 0)
+            scale_x(6)
+            multiply_w2(2, 0, 0)
+            scale_x(7)
+            layer1((0, 1), (1,))
+            widen_x((10, 11), scalar_copy)
+            interleave_w2((2, 0, 0), scalar_copy)
+            layer1((2, 3), (1,))
+            turn_x(8, 9)
+            scale_x(8)
             quantize_x(6)
-            layer1(4, 0)
-            layer1(4, 1)
-            for i in range(8, 12):
-                multiply_x(i)
-                turn_x(i)
-            layer1(6, 0)
-            layer1(6, 1)
-            for i in range(12, 16):
-                multiply_x(i)
-                turn_x(i)
+            scale_x(9)
+            layer1((4, 5))
+            widen_x((12, 13), scalar_copy)
+            relu_w2(2, 0, 1)
             quantize_x(8)
-            relu_w(2, 0, 1)
+            multiply_w2(2, 0, 1)
             quantize_h(0)
-            quantize_h(1)
-            layer1(8, 0)
-            layer1(8, 1)
-            quantize_x(10)
-            sign_w(2, 0, 1)
-            quantize_h(2)
-            interleave_w(2, 0, 1, vector_copy)
-            layer1(10, 0)
-            layer1(10, 1)
-            quantize_x(12)
+            layer1((6, 7))
+            turn_x(10, 11)
+            interleave_w2((2, 0, 1), vector_copy)
             quantize_w(2, 0, 0)
+            scale_x(10)
             quantize_w(2, 0, 1)
-            layer1(12, 0)
-            layer1(12, 1)
+            layer1((8, 9))
+            widen_x((14, 15), scalar_copy)
+            turn_x(12, 13)
+            scale_x(11)
+            quantize_h(2)
+            quantize_x(10)
 
+            layer2(range(0, 4), (0,))
+            scale_x(12)
             quantize_h(4)
+            scale_x(13)
+            layer1((10, 11))
+            relu_w2(2, 1, 0)
+            quantize_x(12)
+            multiply_w2(2, 1, 0)
+            layer2(range(4, 6), (0,))
+            relu_w2(2, 1, 1)
             quantize_h(6)
-            for group in (0, 1, 2, 4):
-                layer2(group, 0)
-            relu_w(2, 1, 0)
-            quantize_x(13)
-            quantize_x(15)
-            layer1(13, 0)
-            layer1(13, 1)
+            multiply_w2(2, 1, 1)
+            layer1((12, 13))
+            interleave_w2((2, 1, 0), vector_copy)
             quantize_h(8)
-            quantize_h(10)
-            sign_w(2, 1, 0)
-            relu_w(2, 1, 1)
-            quantize_h(12)
-            sign_w(2, 1, 1)
-            interleave_w(2, 1, 0, vector_copy)
-            interleave_w(2, 1, 1, vector_copy)
-            for group in (6, 8, 10, 12):
-                layer2(group, 0)
-            quantize_h(13)
-            layer2(13, 0)
-
+            layer2(range(6, 10), (0,))
+            interleave_w2((2, 1, 1), vector_copy)
             quantize_w(2, 1, 0)
+            quantize_h(10)
             quantize_w(2, 1, 1)
-            odd_tiles = range(1, 12, 2)
-            for group in (0, 1, 2, 4, 6, 8, 10):
-                layer2(group, 1, odd_tiles)
-            layer1(15, 0)
-            layer1(15, 1)
+            turn_x(14, 15)
+            layer2(range(10, 12), (0,))
+            scale_x(14, 15)
+            quantize_h(12)
+            quantize_x(14)
+            quantize_x(15)
+
+            odd = [(i, 1) for i in range(3, 16, 2)] + [(14, 1)]
+            layer2(range(0, 4), (1,), odd)
+            layer2(range(12, 14), (0,))
+            layer2(range(4, 6), (1,), odd)
+            layer1((14,))
+            layer2(range(6, 8), (1,), odd)
+            quantize_h(14)
+            layer2(range(8, 10), (1,), odd)
+            layer1((15,))
+            layer2(range(10, 12), (1,), odd)
             quantize_h(15)
-            for group in (12, 13):
-                layer2(group, 1)
-            layer2(15, 0)
-            layer2(15, 1)
+            layer2(range(12, 14), (1,), odd)
+            layer2((14, 15), (0, 1), odd)

@@ -19,6 +19,7 @@ RELU = mybir.ActivationFunctionType.Relu
 P = 128
 PACK = 4
 HALF = P * PACK
+PART = HALF // 2
 BANKS = 8
 
 LOADS = ((0, 2), (2, 2), (4, 2), (6, 2), (8, 4), (12, 4))
@@ -41,11 +42,9 @@ def tile_sparse_connect_kernel(tc, x_bytes, x_scale, th1, sign1, th2, sign2, rel
 
         identity = keep.tile([P, P], F32, name="identity")
         make_identity(nc, identity[:])
-        identity_bf16 = keep.tile([P, P], BF16, name="identity_bf16")
-        make_identity(nc, identity_bf16[:])
         scale = keep.tile([P, 2, PACK], F32, name="scale", align_bytes=64)
 
-        theta, sign, masked, sign_banks, grouped, w_codes, w_scales = {}, {}, {}, {}, {}, {}, {}
+        theta, sign, grouped, w_codes, w_scales = {}, {}, {}, {}, {}
         x_in, x_wide, x_banks, x_grouped, x_codes, x_scales = {}, {}, {}, {}, {}, {}
         h_banks, h_grouped, h_codes, h_scales = {}, {}, {}, {}
         free_banks = list(range(BANKS))
@@ -88,58 +87,33 @@ def tile_sparse_connect_kernel(tc, x_bytes, x_scale, th1, sign1, th2, sign2, rel
                 x_in[first + c] = t[:, c]
 
 
-        def grouped_tile(piece):
-            grouped[piece] = work.tile([P, HALF * PACK], BF16, name="w_grouped", bufs=3, align_bytes=64)
-            return grouped[piece]
-
-        def relu_interleave_theta(*piece):
-            t = work.tile([P, HALF, PACK], BF16, name="w_masked", bufs=2, align_bytes=64)
-            nc.scalar.activation(
-                out=t[:].rearrange("p (c i) j -> p c j i", i=4),
-                in_=theta[piece].rearrange("p j (c i) -> p c j i", i=4),
-                func=RELU,
-            )
-            masked[piece] = t
-
-        def interleave_sign(*piece):
-            sign_banks[piece] = []
-            for b in (0, 1):
-                bank, number = take_bank([P, 2, P, PACK], BF16, "sign_bank")
-                for q in (0, 1):
-                    cols = slice((2 * b + q) * P, (2 * b + q + 1) * P)
-                    nc.tensor.matmul(
-                        out=bank[:, q].rearrange("p c j -> p (c j)"),
-                        lhsT=identity_bf16[:],
-                        rhs=sign[piece][:, :, cols].rearrange("p j c -> p c j"),
-                        start=True,
-                        stop=True,
-                    )
-                sign_banks[piece].append((bank, number))
-
-        def multiply_w1(*piece):
-            w = grouped_tile(piece)
-            for b, (bank, number) in enumerate(sign_banks[piece]):
-                nc.vector.tensor_tensor(
-                    out=w[:].rearrange("p (t m j) -> p t m j", t=PACK, j=PACK)[:, :, b * 64 : (b + 1) * 64],
-                    in0=bank[:].rearrange("p q (m t) j -> p t (q m) j", t=PACK),
-                    in1=masked[piece][:, b * 256 : (b + 1) * 256].rearrange("p (m t) j -> p t m j", t=PACK),
-                    op=MULT,
-                )
-                free_banks.append(number)
-
-        def relu_w2(*piece):
+        def relu_w(*piece):
             th = theta[piece]
             nc.vector.tensor_scalar(out=th, in0=th, scalar1=0.0, scalar2=None, op0=MAX)
 
-        def multiply_w2(*piece):
-            th = theta[piece]
-            nc.vector.tensor_tensor(out=th, in0=th, in1=sign[piece], op=MULT)
+        def multiply_w(piece, parts):
+            for b in parts:
+                cols = slice(b * PART, (b + 1) * PART)
+                th = theta[piece][:, :, cols]
+                nc.vector.tensor_tensor(out=th, in0=th, in1=sign[piece][:, :, cols], op=MULT)
 
-        def interleave_w2(piece, copy):
-            copy(
-                out=grouped_tile(piece)[:].rearrange("p (c i j) -> p c j i", i=4, j=PACK),
-                in_=theta[piece].rearrange("p j (c i) -> p c j i", i=4),
-            )
+        def interleave_w(piece, parts, copy):
+            if piece not in grouped:
+                grouped[piece] = work.tile([P, HALF * PACK], BF16, name="w_grouped", bufs=3, align_bytes=64)
+            w = grouped[piece][:]
+            for b in parts:
+                th = theta[piece][:, :, b * PART : (b + 1) * PART]
+                if piece[0] == 1:
+                    rows = slice(b * PART // PACK, (b + 1) * PART // PACK)
+                    copy(
+                        out=w.rearrange("p (t m j) -> p m t j", t=PACK, j=PACK)[:, rows],
+                        in_=th.rearrange("p j (m t) -> p m t j", t=PACK),
+                    )
+                else:
+                    copy(
+                        out=w[:, b * PART * PACK : (b + 1) * PART * PACK].rearrange("p (c i j) -> p c j i", i=4, j=PACK),
+                        in_=th.rearrange("p j (c i) -> p c j i", i=4),
+                    )
 
         def quantize_w(*piece):
             layer, half, g = piece
@@ -268,122 +242,121 @@ def tile_sparse_connect_kernel(tc, x_bytes, x_scale, th1, sign1, th2, sign2, rel
 
         with tc.manual_schedule():
             nc.scalar.dma_start(out=scale[:], in_=x_scale.rearrange("a b (g p t) -> p (a b g) t", g=2, t=PACK))
-            for half in (0, 1):
-                for g in (0, 1):
-                    load_w1(theta_hbm, theta, half, g)
-                    if (half, g) == (0, 0):
-                        load_x(*LOADS[0])
-                    if (half, g) == (0, 1):
-                        load_x(*LOADS[1])
-                    load_w1(sign_hbm, sign, half, g)
-                    if (half, g) == (1, 0):
-                        load_x(*LOADS[2])
-            load_x(*LOADS[3])
+            load_x(*LOADS[0])
+            for half, g in ((0, 0), (0, 1), (1, 0), (1, 1)):
+                load_w1(theta_hbm, theta, half, g)
+                load_w1(sign_hbm, sign, half, g)
+                if (half, g) != (0, 0):
+                    load_x(*LOADS[2 * half + g])
             load_x(*LOADS[4])
             for g in (0, 1):
                 load_w2(theta_hbm, theta, g)
                 load_w2(sign_hbm, sign, g)
             load_x(*LOADS[5])
 
-            widen_x((0, 1), vector_copy)
-            relu_interleave_theta(1, 0, 0)
+            a, b, c, e = (1, 0, 0), (1, 0, 1), (1, 1, 0), (1, 1, 1)
+            p, q, r, s = (2, 0, 0), (2, 0, 1), (2, 1, 0), (2, 1, 1)
+            widen_x((0,), vector_copy)
+            widen_x((1,), scalar_copy)
             turn_x(0, 1)
-            interleave_sign(1, 0, 0)
-            scale_x(0, 1)
-            relu_interleave_theta(1, 0, 1)
-            multiply_w1(1, 0, 0)
+            relu_w(*a)
+            scale_x(0)
+            multiply_w(a, (0, 1))
+            interleave_w(a, (0, 1), scalar_copy)
+            relu_w(*b)
+            scale_x(1)
+            multiply_w(b, (0, 1))
             quantize_x(0)
-            interleave_sign(1, 0, 1)
-            quantize_w(1, 0, 0)
             widen_x((2, 3), scalar_copy)
             turn_x(2, 3)
-            multiply_w1(1, 0, 1)
+            interleave_w(b, (0, 1), scalar_copy)
+            quantize_w(*a)
+            relu_w(*c)
             scale_x(2)
-            quantize_w(1, 0, 1)
-            relu_interleave_theta(1, 1, 0)
-            interleave_sign(1, 1, 0)
+            multiply_w(c, (0,))
             scale_x(3)
-            widen_x((4, 5), scalar_copy)
-            relu_interleave_theta(1, 1, 1)
-            widen_x((6, 7, 8, 9), scalar_copy)
-            multiply_layer1((0,), (0,))
-            multiply_w1(1, 1, 0)
+            multiply_w(c, (1,))
+            quantize_w(*b)
             quantize_x(2)
+            widen_x((4, 5), scalar_copy)
             turn_x(4, 5)
-            multiply_layer1((1,), (0,))
+            interleave_w(c, (0, 1), scalar_copy)
+            widen_x((6, 7), scalar_copy)
+            multiply_layer1((0, 1, 2, 3), (0,))
             scale_x(4)
-            quantize_w(1, 1, 0)
-            interleave_sign(1, 1, 1)
-            multiply_w1(1, 1, 1)
-            multiply_layer1((2, 3), (0,))
+            relu_w(*e)
             scale_x(5)
-            quantize_w(1, 1, 1)
+            multiply_w(e, (0,))
             quantize_x(4)
+            multiply_w(e, (1,))
             turn_x(6, 7)
-            empty_layer1(range(4), (0,))
-
-            relu_w2(2, 0, 0)
-            scale_x(6)
-            multiply_w2(2, 0, 0)
-            scale_x(7)
-            layer1((0, 1), (1,))
-            widen_x((10, 11), scalar_copy)
-            interleave_w2((2, 0, 0), scalar_copy)
-            layer1((2, 3), (1,))
+            empty_layer1((0, 1), (0,))
+            widen_x((8, 9), scalar_copy)
+            multiply_layer1((4,), (0,))
             turn_x(8, 9)
-            scale_x(8)
+            multiply_layer1((5,), (0,))
+            interleave_w(e, (0,), scalar_copy)
+            quantize_w(*c)
+            interleave_w(e, (1,), vector_copy)
+            scale_x(6)
+            quantize_w(*e)
+            empty_layer1((2, 3, 4, 5), (0,))
+            widen_x((10, 11), scalar_copy)
+            scale_x(7)
+            relu_w(*p)
             quantize_x(6)
-            scale_x(9)
-            layer1((4, 5))
+            multiply_w(p, (0, 1))
+            layer1((0, 1), (1,))
+            interleave_w(p, (0,), scalar_copy)
+            scale_x(8, 9)
+            layer1((2, 3, 4, 5), (1,))
             widen_x((12, 13), scalar_copy)
-            relu_w2(2, 0, 1)
+            relu_w(*q)
             quantize_x(8)
-            multiply_w2(2, 0, 1)
-            quantize_h(0)
-            layer1((6, 7))
             turn_x(10, 11)
-            interleave_w2((2, 0, 1), vector_copy)
-            quantize_w(2, 0, 0)
-            scale_x(10)
-            quantize_w(2, 0, 1)
-            layer1((8, 9))
-            widen_x((14, 15), scalar_copy)
-            turn_x(12, 13)
-            scale_x(11)
-            quantize_h(2)
+            layer1((6,))
+            interleave_w(p, (1,), scalar_copy)
+            layer1((7,))
+            scale_x(10, 11)
+            multiply_w(q, (0,))
             quantize_x(10)
-
-            layer2(range(0, 4), (0,))
-            scale_x(12)
-            quantize_h(4)
-            scale_x(13)
-            layer1((10, 11))
-            relu_w2(2, 1, 0)
+            multiply_w(q, (1,))
+            turn_x(12, 13)
+            layer1((8, 9))
+            scale_x(12, 13)
+            interleave_w(q, (0,), vector_copy)
             quantize_x(12)
-            multiply_w2(2, 1, 0)
-            layer2(range(4, 6), (0,))
-            relu_w2(2, 1, 1)
-            quantize_h(6)
-            multiply_w2(2, 1, 1)
+            interleave_w(q, (1,), vector_copy)
+            quantize_w(*p)
+            quantize_h(0)
+            quantize_w(*q)
+            layer1((10, 11))
+            quantize_h(2)
+            quantize_h(4)
             layer1((12, 13))
-            interleave_w2((2, 1, 0), vector_copy)
+            relu_w(*r)
+            quantize_h(6)
+            relu_w(*s)
+            multiply_w(r, (0, 1))
             quantize_h(8)
-            layer2(range(6, 10), (0,))
-            interleave_w2((2, 1, 1), vector_copy)
-            quantize_w(2, 1, 0)
+            multiply_w(s, (0, 1))
+            interleave_w(r, (0, 1), vector_copy)
             quantize_h(10)
-            quantize_w(2, 1, 1)
-            turn_x(14, 15)
-            layer2(range(10, 12), (0,))
-            scale_x(14, 15)
+            interleave_w(s, (0,), vector_copy)
             quantize_h(12)
+            interleave_w(s, (1,), vector_copy)
+            quantize_w(*r)
+            quantize_w(*s)
+            layer2(range(0, 4), (0,))
+            widen_x((14, 15), scalar_copy)
+            layer2(range(4, 10), (0,))
+            turn_x(14, 15)
+            layer2(range(10, 14), (0,))
+            scale_x(14, 15)
             quantize_x(14)
             quantize_x(15)
-
-            odd = [(i, 1) for i in range(3, 16, 2)] + [(14, 1)]
-            layer2(range(0, 4), (1,), odd)
-            layer2(range(12, 14), (0,))
-            layer2(range(4, 6), (1,), odd)
+            odd = [(i, 1) for i in range(5, 16, 2)] + [(14, 1)]
+            layer2(range(0, 6), (1,), odd)
             layer1((14,))
             layer2(range(6, 8), (1,), odd)
             quantize_h(14)

@@ -106,8 +106,8 @@ def tile_sparse_connect_kernel(tc, x_bytes, x_scale, th1, sign1, th2, sign2, rel
                 if piece[0] == 1:
                     rows = slice(b * PART // PACK, (b + 1) * PART // PACK)
                     copy(
-                        out=w.rearrange("p (t m j) -> p m t j", t=PACK, j=PACK)[:, rows],
-                        in_=th.rearrange("p j (m t) -> p m t j", t=PACK),
+                        out=w.rearrange("p (t m j) -> p m j t", t=PACK, j=PACK)[:, rows],
+                        in_=th.rearrange("p j (m t) -> p m j t", t=PACK),
                     )
                 else:
                     copy(

@@ -14,6 +14,7 @@ FP8 = mybir.dt.float8_e4m3fn
 FP8X4 = mybir.dt.float8_e4m3fn_x4
 MAX = mybir.AluOpType.max
 MULT = mybir.AluOpType.mult
+ADD = mybir.AluOpType.add
 RELU = mybir.ActivationFunctionType.Relu
 
 P = 128
@@ -22,8 +23,9 @@ HALF = P * PACK
 PART = HALF // 2
 BANKS = 8
 
-LOADS = ((0, 2), (2, 2), (4, 2), (6, 2), (8, 4), (12, 4))
-GROUPS = ((0, 2), (2, 2), (4, 2), (6, 2), (8, 2), (10, 2), (12, 2), (14, 1), (15, 1))
+LOADS = ((0, 2), (2, 2), (4, 4), (8, 4), (12, 4))
+X_GROUPS = ((0, 2), (2, 2), (4, 2), (6, 2), (8, 2), (10, 2), (12, 2), (14, 1), (15, 1))
+H_GROUPS = ((0, 4), (4, 4), (8, 4), (12, 2), (14, 1), (15, 1))
 
 
 def tile_sparse_connect_kernel(tc, x_bytes, x_scale, th1, sign1, th2, sign2, relu, out):
@@ -33,7 +35,7 @@ def tile_sparse_connect_kernel(tc, x_bytes, x_scale, th1, sign1, th2, sign2, rel
     out_rows = out.flatten_outer_dims()
     theta_hbm = {n: a.rearrange("(g p j) f -> g p j f", p=P, j=PACK) for n, a in ((1, th1), (2, th2))}
     sign_hbm = {n: a.rearrange("(g p j) f -> g p j f", p=P, j=PACK) for n, a in ((1, sign1), (2, sign2))}
-    group_size = dict(GROUPS)
+    x_group_size, h_group_size = dict(X_GROUPS), dict(H_GROUPS)
 
     with ExitStack() as ctx:
         keep = ctx.enter_context(tc.tile_pool(name="keep", bufs=1))
@@ -54,13 +56,10 @@ def tile_sparse_connect_kernel(tc, x_bytes, x_scale, th1, sign1, th2, sign2, rel
             free_banks.remove(number)
             return psum.tile(shape, dtype, name=name, tag=f"bank{number}"), number
 
-        def tiles_of(group):
-            return range(group, group + group_size[group])
+        def group_of(i, groups):
+            return max(first for first, count in groups if first <= i)
 
-        def group_of(i):
-            return max(first for first, count in GROUPS if first <= i)
-
-        def relu_out_of_psum(out, in_, on_vector):
+        def relu_on(out, in_, on_vector):
             if on_vector:
                 nc.vector.tensor_scalar(out=out, in0=in_, scalar1=0.0, scalar2=None, op0=MAX)
             else:
@@ -87,33 +86,41 @@ def tile_sparse_connect_kernel(tc, x_bytes, x_scale, th1, sign1, th2, sign2, rel
                 x_in[first + c] = t[:, c]
 
 
-        def relu_w(*piece):
-            th = theta[piece]
-            nc.vector.tensor_scalar(out=th, in0=th, scalar1=0.0, scalar2=None, op0=MAX)
+        def relu_w(piece, on_vector):
+            relu_on(theta[piece], theta[piece], on_vector)
 
-        def multiply_w(piece, parts):
-            for b in parts:
-                cols = slice(b * PART, (b + 1) * PART)
-                th = theta[piece][:, :, cols]
-                nc.vector.tensor_tensor(out=th, in0=th, in1=sign[piece][:, :, cols], op=MULT)
+        def multiply_w(piece, cols=slice(0, HALF)):
+            th = theta[piece][:, :, cols]
+            nc.vector.tensor_tensor(out=th, in0=th, in1=sign[piece][:, :, cols], op=MULT)
 
-        def interleave_w(piece, parts, copy):
+        def grouped_tile(piece):
             if piece not in grouped:
                 grouped[piece] = work.tile([P, HALF * PACK], BF16, name="w_grouped", bufs=3, align_bytes=64)
-            w = grouped[piece][:]
-            for b in parts:
-                th = theta[piece][:, :, b * PART : (b + 1) * PART]
-                if piece[0] == 1:
-                    rows = slice(b * PART // PACK, (b + 1) * PART // PACK)
-                    copy(
-                        out=w.rearrange("p (t m j) -> p m j t", t=PACK, j=PACK)[:, rows],
-                        in_=th.rearrange("p j (m t) -> p m j t", t=PACK),
-                    )
-                else:
-                    copy(
-                        out=w[:, b * PART * PACK : (b + 1) * PART * PACK].rearrange("p (c i j) -> p c j i", i=4, j=PACK),
-                        in_=th.rearrange("p j (c i) -> p c j i", i=4),
-                    )
+            return grouped[piece][:]
+
+        def interleave_w1(piece, cols=slice(0, HALF)):
+            nc.scalar.copy(
+                out=grouped_tile(piece).rearrange("p (t m j) -> p m j t", t=PACK, j=PACK)[
+                    :, cols.start // PACK : cols.stop // PACK
+                ],
+                in_=theta[piece][:, :, cols].rearrange("p j (m t) -> p m j t", t=PACK),
+            )
+
+        def interleave_w2_vector(piece):
+            nc.vector.tensor_copy(
+                out=grouped_tile(piece).rearrange("p (c i j) -> p c j i", i=4, j=PACK),
+                in_=theta[piece].rearrange("p j (c i) -> p c j i", i=4),
+            )
+
+        def interleave_w2_gpsimd(piece, cols):
+            nc.gpsimd.tensor_scalar(
+                out=grouped_tile(piece).rearrange("p (c j) -> p c j", j=PACK)[:, cols],
+                in0=theta[piece][:, :, cols].rearrange("p j c -> p c j"),
+                scalar1=1.0,
+                scalar2=0.0,
+                op0=MULT,
+                op1=ADD,
+            )
 
         def quantize_w(*piece):
             layer, half, g = piece
@@ -125,7 +132,7 @@ def tile_sparse_connect_kernel(tc, x_bytes, x_scale, th1, sign1, th2, sign2, rel
 
         def widen_x(tiles, copy):
             for i in tiles:
-                x_wide[i] = work.tile([P, D], BF16, name="x_wide", bufs=6, align_bytes=64)
+                x_wide[i] = work.tile([P, D], BF16, name="x_wide", bufs=8, align_bytes=64)
                 copy(out=x_wide[i][:], in_=x_in[i].bitcast(FP8))
 
         def turn_x(*tiles):
@@ -139,9 +146,11 @@ def tile_sparse_connect_kernel(tc, x_bytes, x_scale, th1, sign1, th2, sign2, rel
 
         def scale_x(*tiles):
             for i in tiles:
-                group = group_of(i)
+                group = group_of(i, X_GROUPS)
                 if i == group:
-                    x_grouped[group] = work.tile([P, group_size[group], D], BF16, name="x_grouped", bufs=3, align_bytes=64)
+                    x_grouped[group] = work.tile(
+                        [P, x_group_size[group], D], BF16, name="x_grouped", bufs=3, align_bytes=64
+                    )
                 bank, number = x_banks[i]
                 values = bank[:].rearrange("p u g r -> p (u g r)").bitcast(BF16)
                 nc.vector.tensor_tensor(
@@ -153,16 +162,16 @@ def tile_sparse_connect_kernel(tc, x_bytes, x_scale, th1, sign1, th2, sign2, rel
                 free_banks.append(number)
 
         def quantize_x(group):
-            count = group_size[group]
-            codes = work.tile([P, count, 2, P], U32, name="x_codes", bufs=5, align_bytes=64)
-            scales = work.tile([P, count, 2, P], U8, name="x_scales", bufs=5, align_bytes=64)
+            count = x_group_size[group]
+            codes = work.tile([P, count, 2, P], U32, name="x_codes", bufs=6, align_bytes=64)
+            scales = work.tile([P, count, 2, P], U8, name="x_scales", bufs=6, align_bytes=64)
             nc.vector.quantize_mx(
                 out=codes[:].rearrange("p c g r -> p (c g r)").bitcast(FP8X4),
                 scales=scales[:].rearrange("p c g r -> p (c g r)"),
                 in_=x_grouped[group][:].rearrange("p c d -> p (c d)"),
             )
-            for c, i in enumerate(tiles_of(group)):
-                x_codes[i], x_scales[i] = codes[:, c], scales[:, c]
+            for c in range(count):
+                x_codes[group + c], x_scales[group + c] = codes[:, c], scales[:, c]
 
 
         def multiply_layer1(tiles, halves):
@@ -185,10 +194,10 @@ def tile_sparse_connect_kernel(tc, x_bytes, x_scale, th1, sign1, th2, sign2, rel
 
         def empty_layer1(tiles, halves):
             for i in tiles:
-                group = group_of(i)
+                group = group_of(i, H_GROUPS)
                 if group not in h_grouped:
-                    h_grouped[group] = work.tile(
-                        [P, group_size[group], 2, P, PACK], BF16, name="h_grouped", bufs=7, align_bytes=64
+                    h_grouped[group] = keep.tile(
+                        [P, h_group_size[group], 2, P, PACK], BF16, name=f"h_grouped{group}", align_bytes=64
                     )
                 for half in halves:
                     bank, number = h_banks[i, half]
@@ -204,7 +213,7 @@ def tile_sparse_connect_kernel(tc, x_bytes, x_scale, th1, sign1, th2, sign2, rel
                     empty_layer1((i,), (half,))
 
         def quantize_h(group):
-            count = group_size[group]
+            count = h_group_size[group]
             codes = keep.tile([P, count, 2, P], U32, name=f"h_codes{group}", align_bytes=64)
             scales = keep.tile([P, count, 2, P], U8, name=f"h_scales{group}", align_bytes=64)
             nc.vector.quantize_mx(
@@ -212,8 +221,8 @@ def tile_sparse_connect_kernel(tc, x_bytes, x_scale, th1, sign1, th2, sign2, rel
                 scales=scales[:].rearrange("p c g n -> p (c g n)"),
                 in_=h_grouped[group][:].rearrange("p c g n t -> p (c g n t)"),
             )
-            for c, i in enumerate(tiles_of(group)):
-                h_codes[i], h_scales[i] = codes[:, c], scales[:, c]
+            for c in range(count):
+                h_codes[group + c], h_scales[group + c] = codes[:, c], scales[:, c]
 
 
         def layer2(tiles, halves, on_vector=()):
@@ -231,7 +240,7 @@ def tile_sparse_connect_kernel(tc, x_bytes, x_scale, th1, sign1, th2, sign2, rel
                             stop=(g == 1),
                         )
                     result = work.tile([P, HALF], F32, name="result", bufs=8, align_bytes=64)
-                    relu_out_of_psum(result[:], bank[:], (i, half) in on_vector)
+                    relu_on(result[:], bank[:], (i, half) in on_vector)
                     free_banks.append(number)
                     first, count = max(load for load in LOADS if load[0] <= i)
                     rows = out_rows[first * P : (first + count) * P, :].rearrange("(p c) n -> c p n", c=count)
@@ -243,120 +252,112 @@ def tile_sparse_connect_kernel(tc, x_bytes, x_scale, th1, sign1, th2, sign2, rel
         with tc.manual_schedule():
             nc.scalar.dma_start(out=scale[:], in_=x_scale.rearrange("a b (g p t) -> p (a b g) t", g=2, t=PACK))
             load_x(*LOADS[0])
+            load_x(*LOADS[1])
             for half, g in ((0, 0), (0, 1), (1, 0), (1, 1)):
                 load_w1(theta_hbm, theta, half, g)
                 load_w1(sign_hbm, sign, half, g)
-                if (half, g) != (0, 0):
-                    load_x(*LOADS[2 * half + g])
-            load_x(*LOADS[4])
+                if (half, g) == (0, 0):
+                    load_x(*LOADS[2])
+            load_x(*LOADS[3])
             for g in (0, 1):
                 load_w2(theta_hbm, theta, g)
                 load_w2(sign_hbm, sign, g)
-            load_x(*LOADS[5])
+            load_x(*LOADS[4])
 
             a, b, c, e = (1, 0, 0), (1, 0, 1), (1, 1, 0), (1, 1, 1)
             p, q, r, s = (2, 0, 0), (2, 0, 1), (2, 1, 0), (2, 1, 1)
-            widen_x((0,), vector_copy)
-            widen_x((1,), scalar_copy)
-            turn_x(0, 1)
-            relu_w(*a)
-            scale_x(0)
-            multiply_w(a, (0, 1))
-            interleave_w(a, (0, 1), scalar_copy)
-            relu_w(*b)
-            scale_x(1)
-            multiply_w(b, (0, 1))
-            quantize_x(0)
-            widen_x((2, 3), scalar_copy)
-            turn_x(2, 3)
-            interleave_w(b, (0, 1), scalar_copy)
-            quantize_w(*a)
-            relu_w(*c)
-            scale_x(2)
-            multiply_w(c, (0,))
-            scale_x(3)
-            multiply_w(c, (1,))
-            quantize_w(*b)
-            quantize_x(2)
-            widen_x((4, 5), scalar_copy)
+            left, right = slice(0, PART), slice(PART, HALF)
+            widen_x((0, 1, 2, 3), scalar_copy)
+            turn_x(0, 1, 2, 3)
+            relu_w(a, False)
+            scale_x(0, 1, 2)
+            multiply_w(a)
+            widen_x((4, 5, 6), scalar_copy)
             turn_x(4, 5)
-            interleave_w(c, (0, 1), scalar_copy)
-            widen_x((6, 7), scalar_copy)
-            multiply_layer1((0, 1, 2, 3), (0,))
-            scale_x(4)
-            relu_w(*e)
-            scale_x(5)
-            multiply_w(e, (0,))
-            quantize_x(4)
-            multiply_w(e, (1,))
+            interleave_w1(a)
+            widen_x((7,), scalar_copy)
+            relu_w(b, True)
+            quantize_x(0)
+            multiply_w(b)
             turn_x(6, 7)
-            empty_layer1((0, 1), (0,))
-            widen_x((8, 9), scalar_copy)
-            multiply_layer1((4,), (0,))
-            turn_x(8, 9)
-            multiply_layer1((5,), (0,))
-            interleave_w(e, (0,), scalar_copy)
+            interleave_w1(b)
+            relu_w(c, True)
+            quantize_w(*a)
+            multiply_w(c)
+            interleave_w1(c)
+            scale_x(3)
+            relu_w(e, True)
+            quantize_w(*b)
+            multiply_w(e)
+            quantize_x(2)
+            multiply_layer1((0, 1), (0,))
+            interleave_w1(e)
+            multiply_layer1((2, 3), (0,))
+            scale_x(4)
             quantize_w(*c)
-            interleave_w(e, (1,), vector_copy)
-            scale_x(6)
+            scale_x(5)
             quantize_w(*e)
-            empty_layer1((2, 3, 4, 5), (0,))
+            empty_layer1((0, 1, 2, 3), (0,))
+            widen_x((8, 9), scalar_copy)
+            relu_w(p, True)
+            quantize_x(4)
+            multiply_w(p, left)
+            interleave_w2_gpsimd(p, left)
+            layer1((0, 1, 2, 3), (1,))
+            scale_x(6, 7)
             widen_x((10, 11), scalar_copy)
-            scale_x(7)
-            relu_w(*p)
+            relu_w(q, True)
             quantize_x(6)
-            multiply_w(p, (0, 1))
-            layer1((0, 1), (1,))
-            interleave_w(p, (0,), scalar_copy)
+            multiply_w(p, right)
+            interleave_w2_gpsimd(p, right)
+            layer1((4,), (0,))
+            turn_x(8, 9)
             scale_x(8, 9)
-            layer1((2, 3, 4, 5), (1,))
+            layer1((4,), (1,))
+            layer1((5,))
             widen_x((12, 13), scalar_copy)
-            relu_w(*q)
-            quantize_x(8)
-            turn_x(10, 11)
-            layer1((6,))
-            interleave_w(p, (1,), scalar_copy)
-            layer1((7,))
-            scale_x(10, 11)
-            multiply_w(q, (0,))
-            quantize_x(10)
-            multiply_w(q, (1,))
-            turn_x(12, 13)
-            layer1((8, 9))
-            scale_x(12, 13)
-            interleave_w(q, (0,), vector_copy)
-            quantize_x(12)
-            interleave_w(q, (1,), vector_copy)
             quantize_w(*p)
+            quantize_x(8)
+            multiply_w(q, left)
+            interleave_w2_gpsimd(q, left)
+            layer1((6,))
+            turn_x(10, 11)
+            scale_x(10, 11)
+            layer1((7,))
+            widen_x((14, 15), scalar_copy)
             quantize_h(0)
+            quantize_x(10)
+            multiply_w(q, right)
+            interleave_w2_gpsimd(q, right)
+            layer1((8,))
+            turn_x(12, 13)
+            layer1((9,))
+            turn_x(14, 15)
+            relu_w(r, False)
+            scale_x(12, 13)
             quantize_w(*q)
+            quantize_x(12)
             layer1((10, 11))
-            quantize_h(2)
             quantize_h(4)
+            multiply_w(r)
+            relu_w(s, True)
+            interleave_w2_vector(r)
+            layer2(range(0, 4), (0,))
             layer1((12, 13))
-            relu_w(*r)
-            quantize_h(6)
-            relu_w(*s)
-            multiply_w(r, (0, 1))
+            multiply_w(s)
             quantize_h(8)
-            multiply_w(s, (0, 1))
-            interleave_w(r, (0, 1), vector_copy)
-            quantize_h(10)
-            interleave_w(s, (0,), vector_copy)
-            quantize_h(12)
-            interleave_w(s, (1,), vector_copy)
+            interleave_w2_vector(s)
             quantize_w(*r)
             quantize_w(*s)
-            layer2(range(0, 4), (0,))
-            widen_x((14, 15), scalar_copy)
-            layer2(range(4, 10), (0,))
-            turn_x(14, 15)
-            layer2(range(10, 14), (0,))
+            quantize_h(12)
+            layer2(range(4, 12), (0,))
             scale_x(14, 15)
             quantize_x(14)
             quantize_x(15)
             odd = [(i, 1) for i in range(5, 16, 2)] + [(14, 1)]
-            layer2(range(0, 6), (1,), odd)
+            layer2(range(0, 2), (1,), odd)
+            layer2(range(12, 14), (0,))
+            layer2(range(2, 6), (1,), odd)
             layer1((14,))
             layer2(range(6, 8), (1,), odd)
             quantize_h(14)

@@ -23,7 +23,7 @@ HALF = P * PACK
 PART = HALF // 2
 BANKS = 8
 
-LOADS = ((0, 2), (2, 2), (4, 4), (8, 4), (12, 4))
+LOADS = ((0, 1), (1, 1), (2, 2), (4, 4), (8, 4), (12, 4))
 X_GROUPS = ((0, 2), (2, 2), (4, 2), (6, 2), (8, 2), (10, 2), (12, 2), (14, 1), (15, 1))
 H_GROUPS = ((0, 4), (4, 4), (8, 4), (12, 2), (14, 1), (15, 1))
 
@@ -98,18 +98,28 @@ def tile_sparse_connect_kernel(tc, x_bytes, x_scale, th1, sign1, th2, sign2, rel
                 grouped[piece] = work.tile([P, HALF * PACK], BF16, name="w_grouped", bufs=3, align_bytes=64)
             return grouped[piece][:]
 
-        def interleave_w1(piece, cols=slice(0, HALF)):
+        def interleave_w1(piece, slots=slice(0, PACK)):
             nc.scalar.copy(
-                out=grouped_tile(piece).rearrange("p (t m j) -> p m j t", t=PACK, j=PACK)[
-                    :, cols.start // PACK : cols.stop // PACK
-                ],
-                in_=theta[piece][:, :, cols].rearrange("p j (m t) -> p m j t", t=PACK),
+                out=grouped_tile(piece).rearrange("p (t m j) -> p m j t", t=PACK, j=PACK)[:, :, :, slots],
+                in_=theta[piece].rearrange("p j (m t) -> p m j t", t=PACK)[:, :, :, slots],
             )
 
-        def interleave_w2_vector(piece):
+        def interleave_w2_vector(piece, cols):
             nc.vector.tensor_copy(
-                out=grouped_tile(piece).rearrange("p (c i j) -> p c j i", i=4, j=PACK),
-                in_=theta[piece].rearrange("p j (c i) -> p c j i", i=4),
+                out=grouped_tile(piece)[:, cols.start * PACK : cols.stop * PACK].rearrange(
+                    "p (c i j) -> p c j i", i=4, j=PACK
+                ),
+                in_=theta[piece][:, :, cols].rearrange("p j (c i) -> p c j i", i=4),
+            )
+
+        def interleave_w1_gpsimd(piece, slots):
+            nc.gpsimd.tensor_scalar(
+                out=grouped_tile(piece).rearrange("p (t m j) -> p m t j", t=PACK, j=PACK)[:, :, slots],
+                in0=theta[piece].rearrange("p j (m t) -> p m t j", t=PACK)[:, :, slots],
+                scalar1=1.0,
+                scalar2=0.0,
+                op0=MULT,
+                op1=ADD,
             )
 
         def interleave_w2_gpsimd(piece, cols):
@@ -122,12 +132,16 @@ def tile_sparse_connect_kernel(tc, x_bytes, x_scale, th1, sign1, th2, sign2, rel
                 op1=ADD,
             )
 
-        def quantize_w(*piece):
-            layer, half, g = piece
-            codes = keep.tile([P, HALF], U32, name=f"w_codes{layer}{half}{g}", align_bytes=64)
-            scales = keep.tile([P, HALF], U8, name=f"w_scales{layer}{half}{g}", align_bytes=64)
-            nc.vector.quantize_mx(out=codes[:].bitcast(FP8X4), scales=scales[:], in_=grouped[piece][:])
-            w_codes[piece], w_scales[piece] = codes, scales
+        def quantize_w(piece, cols=slice(0, HALF)):
+            if piece not in w_codes:
+                layer, half, g = piece
+                w_codes[piece] = keep.tile([P, HALF], U32, name=f"w_codes{layer}{half}{g}", align_bytes=64)
+                w_scales[piece] = keep.tile([P, HALF], U8, name=f"w_scales{layer}{half}{g}", align_bytes=64)
+            nc.vector.quantize_mx(
+                out=w_codes[piece][:, cols].bitcast(FP8X4),
+                scales=w_scales[piece][:, cols],
+                in_=grouped[piece][:, cols.start * PACK : cols.stop * PACK],
+            )
 
 
         def widen_x(tiles, copy):
@@ -225,26 +239,29 @@ def tile_sparse_connect_kernel(tc, x_bytes, x_scale, th1, sign1, th2, sign2, rel
                 h_codes[group + c], h_scales[group + c] = codes[:, c], scales[:, c]
 
 
-        def layer2(tiles, halves, on_vector=()):
+        def layer2_columns(i, half, cols, on_vector):
+            width = cols.stop - cols.start
+            bank, number = take_bank([P, width], F32, "out_bank")
+            for g in (0, 1):
+                nc.tensor.matmul_mx(
+                    out=bank[:],
+                    lhsT=h_codes[i][:, g].bitcast(FP8X4),
+                    lhsT_scale=h_scales[i][:, g],
+                    rhs=w_codes[2, half, g][:, cols].bitcast(FP8X4),
+                    rhs_scale=w_scales[2, half, g][:, cols],
+                    start=(g == 0),
+                    stop=(g == 1),
+                )
+            result = work.tile([P, width], F32, name="result", bufs=8, align_bytes=64)
+            relu_on(result[:], bank[:], on_vector)
+            free_banks.append(number)
+            first, count = max(load for load in LOADS if load[0] <= i)
+            rows = out_rows[first * P : (first + count) * P, :].rearrange("(p c) n -> c p n", c=count)
+            nc.sync.dma_start(out=rows[i - first][:, half * HALF + cols.start : half * HALF + cols.stop], in_=result[:])
+
+        def layer2(tiles, half, cols=slice(0, HALF), on_vector=()):
             for i in tiles:
-                for half in halves:
-                    bank, number = take_bank([P, HALF], F32, "out_bank")
-                    for g in (0, 1):
-                        nc.tensor.matmul_mx(
-                            out=bank[:],
-                            lhsT=h_codes[i][:, g].bitcast(FP8X4),
-                            lhsT_scale=h_scales[i][:, g],
-                            rhs=w_codes[2, half, g][:].bitcast(FP8X4),
-                            rhs_scale=w_scales[2, half, g][:],
-                            start=(g == 0),
-                            stop=(g == 1),
-                        )
-                    result = work.tile([P, HALF], F32, name="result", bufs=8, align_bytes=64)
-                    relu_on(result[:], bank[:], (i, half) in on_vector)
-                    free_banks.append(number)
-                    first, count = max(load for load in LOADS if load[0] <= i)
-                    rows = out_rows[first * P : (first + count) * P, :].rearrange("(p c) n -> c p n", c=count)
-                    nc.sync.dma_start(out=rows[i - first][:, half * HALF : (half + 1) * HALF], in_=result[:])
+                layer2_columns(i, half, cols, i in on_vector)
 
 
         scalar_copy, vector_copy = nc.scalar.copy, nc.vector.tensor_copy
@@ -253,20 +270,20 @@ def tile_sparse_connect_kernel(tc, x_bytes, x_scale, th1, sign1, th2, sign2, rel
             nc.scalar.dma_start(out=scale[:], in_=x_scale.rearrange("a b (g p t) -> p (a b g) t", g=2, t=PACK))
             load_x(*LOADS[0])
             load_x(*LOADS[1])
+            load_x(*LOADS[2])
             for half, g in ((0, 0), (0, 1), (1, 0), (1, 1)):
                 load_w1(theta_hbm, theta, half, g)
                 load_w1(sign_hbm, sign, half, g)
                 if (half, g) == (0, 0):
-                    load_x(*LOADS[2])
-            load_x(*LOADS[3])
+                    load_x(*LOADS[3])
             for g in (0, 1):
                 load_w2(theta_hbm, theta, g)
                 load_w2(sign_hbm, sign, g)
-            load_x(*LOADS[4])
+                load_x(*LOADS[4 + g])
 
             a, b, c, e = (1, 0, 0), (1, 0, 1), (1, 1, 0), (1, 1, 1)
             p, q, r, s = (2, 0, 0), (2, 0, 1), (2, 1, 0), (2, 1, 1)
-            left, right = slice(0, PART), slice(PART, HALF)
+            whole, left, right = slice(0, HALF), slice(0, PART), slice(PART, HALF)
             widen_x((0, 1, 2, 3), scalar_copy)
             turn_x(0, 1, 2, 3)
             relu_w(a, False)
@@ -276,47 +293,46 @@ def tile_sparse_connect_kernel(tc, x_bytes, x_scale, th1, sign1, th2, sign2, rel
             turn_x(4, 5)
             interleave_w1(a)
             widen_x((7,), scalar_copy)
+            scale_x(3)
             relu_w(b, True)
             quantize_x(0)
             multiply_w(b)
             turn_x(6, 7)
             interleave_w1(b)
+            scale_x(4)
             relu_w(c, True)
-            quantize_w(*a)
+            quantize_w(a)
             multiply_w(c)
             interleave_w1(c)
-            scale_x(3)
+            quantize_w(b)
             relu_w(e, True)
-            quantize_w(*b)
-            multiply_w(e)
             quantize_x(2)
-            multiply_layer1((0, 1), (0,))
+            multiply_layer1((0, 1, 2, 3), (0,))
+            empty_layer1((0,), (0,))
+            multiply_w(e)
             interleave_w1(e)
-            multiply_layer1((2, 3), (0,))
-            scale_x(4)
-            quantize_w(*c)
             scale_x(5)
-            quantize_w(*e)
-            empty_layer1((0, 1, 2, 3), (0,))
-            widen_x((8, 9), scalar_copy)
-            relu_w(p, True)
+            quantize_w(c)
             quantize_x(4)
+            relu_w(p, True)
+            multiply_layer1((4,), (0,))
+            quantize_w(e)
+            empty_layer1((1, 2, 3, 4), (0,))
+            widen_x((8, 9), scalar_copy)
             multiply_w(p, left)
             interleave_w2_gpsimd(p, left)
             layer1((0, 1, 2, 3), (1,))
             scale_x(6, 7)
             widen_x((10, 11), scalar_copy)
-            relu_w(q, True)
             quantize_x(6)
             multiply_w(p, right)
             interleave_w2_gpsimd(p, right)
-            layer1((4,), (0,))
             turn_x(8, 9)
-            scale_x(8, 9)
             layer1((4,), (1,))
             layer1((5,))
+            scale_x(8, 9)
             widen_x((12, 13), scalar_copy)
-            quantize_w(*p)
+            relu_w(q, True)
             quantize_x(8)
             multiply_w(q, left)
             interleave_w2_gpsimd(q, left)
@@ -325,7 +341,7 @@ def tile_sparse_connect_kernel(tc, x_bytes, x_scale, th1, sign1, th2, sign2, rel
             scale_x(10, 11)
             layer1((7,))
             widen_x((14, 15), scalar_copy)
-            quantize_h(0)
+            quantize_w(p)
             quantize_x(10)
             multiply_w(q, right)
             interleave_w2_gpsimd(q, right)
@@ -333,37 +349,41 @@ def tile_sparse_connect_kernel(tc, x_bytes, x_scale, th1, sign1, th2, sign2, rel
             turn_x(12, 13)
             layer1((9,))
             turn_x(14, 15)
-            relu_w(r, False)
             scale_x(12, 13)
-            quantize_w(*q)
-            quantize_x(12)
-            layer1((10, 11))
-            quantize_h(4)
-            multiply_w(r)
             relu_w(s, True)
-            interleave_w2_vector(r)
-            layer2(range(0, 4), (0,))
-            layer1((12, 13))
+            quantize_x(12)
+            quantize_w(q)
+            relu_w(r, True)
+            quantize_h(0)
+            layer1((10, 11))
+            multiply_w(r)
+            quantize_h(4)
+            interleave_w2_vector(r, whole)
+            layer1((12,))
+            layer2(range(0, 4), 0)
+            layer1((13,))
             multiply_w(s)
             quantize_h(8)
-            interleave_w2_vector(s)
-            quantize_w(*r)
-            quantize_w(*s)
+            interleave_w2_vector(s, whole)
+            quantize_w(r)
+            quantize_w(s)
             quantize_h(12)
-            layer2(range(4, 12), (0,))
+            layer2(range(4, 12), 0)
             scale_x(14, 15)
             quantize_x(14)
             quantize_x(15)
-            odd = [(i, 1) for i in range(5, 16, 2)] + [(14, 1)]
-            layer2(range(0, 2), (1,), odd)
-            layer2(range(12, 14), (0,))
-            layer2(range(2, 6), (1,), odd)
+            odd = range(5, 16, 2)
+            layer2(range(0, 2), 1, whole, odd)
+            layer2(range(12, 14), 0)
+            layer2(range(2, 6), 1, whole, odd)
             layer1((14,))
-            layer2(range(6, 8), (1,), odd)
+            layer2(range(6, 8), 1, whole, odd)
             quantize_h(14)
-            layer2(range(8, 10), (1,), odd)
+            layer2(range(8, 10), 1, whole, odd)
             layer1((15,))
-            layer2(range(10, 12), (1,), odd)
+            layer2(range(10, 12), 1, whole, odd)
             quantize_h(15)
-            layer2(range(12, 14), (1,), odd)
-            layer2((14, 15), (0, 1), odd)
+            layer2(range(12, 14), 1, whole, odd)
+            for i in (14, 15):
+                layer2((i,), 0)
+                layer2((i,), 1, whole, (i,))

@@ -98,10 +98,12 @@ def tile_sparse_connect_kernel(tc, x_bytes, x_scale, th1, sign1, th2, sign2, rel
                 grouped[piece] = work.tile([P, HALF * PACK], BF16, name="w_grouped", bufs=3, align_bytes=64)
             return grouped[piece][:]
 
-        def interleave_w1(piece, slots=slice(0, PACK)):
-            nc.scalar.copy(
-                out=grouped_tile(piece).rearrange("p (t m j) -> p m j t", t=PACK, j=PACK)[:, :, :, slots],
-                in_=theta[piece].rearrange("p j (m t) -> p m j t", t=PACK)[:, :, :, slots],
+        def interleave_w1(piece, cols, copy):
+            copy(
+                out=grouped_tile(piece).rearrange("p (t m j) -> p m j t", t=PACK, j=PACK)[
+                    :, cols.start // PACK : cols.stop // PACK
+                ],
+                in_=theta[piece][:, :, cols].rearrange("p j (m t) -> p m j t", t=PACK),
             )
 
         def interleave_w2_vector(piece, cols):
@@ -110,16 +112,6 @@ def tile_sparse_connect_kernel(tc, x_bytes, x_scale, th1, sign1, th2, sign2, rel
                     "p (c i j) -> p c j i", i=4, j=PACK
                 ),
                 in_=theta[piece][:, :, cols].rearrange("p j (c i) -> p c j i", i=4),
-            )
-
-        def interleave_w1_gpsimd(piece, slots):
-            nc.gpsimd.tensor_scalar(
-                out=grouped_tile(piece).rearrange("p (t m j) -> p m t j", t=PACK, j=PACK)[:, :, slots],
-                in0=theta[piece].rearrange("p j (m t) -> p m t j", t=PACK)[:, :, slots],
-                scalar1=1.0,
-                scalar2=0.0,
-                op0=MULT,
-                op1=ADD,
             )
 
         def interleave_w2_gpsimd(piece, cols):
@@ -291,48 +283,47 @@ def tile_sparse_connect_kernel(tc, x_bytes, x_scale, th1, sign1, th2, sign2, rel
             multiply_w(a)
             widen_x((4, 5, 6), scalar_copy)
             turn_x(4, 5)
-            interleave_w1(a)
+            interleave_w1(a, whole, scalar_copy)
             widen_x((7,), scalar_copy)
             scale_x(3)
             relu_w(b, True)
             quantize_x(0)
             multiply_w(b)
             turn_x(6, 7)
-            interleave_w1(b)
+            interleave_w1(b, whole, scalar_copy)
             scale_x(4)
             relu_w(c, True)
             quantize_w(a)
             multiply_w(c)
-            interleave_w1(c)
-            quantize_w(b)
+            interleave_w1(c, whole, scalar_copy)
             relu_w(e, True)
-            quantize_x(2)
-            multiply_layer1((0, 1, 2, 3), (0,))
-            empty_layer1((0,), (0,))
+            quantize_w(b)
             multiply_w(e)
-            interleave_w1(e)
-            scale_x(5)
+            quantize_x(2)
+            interleave_w1(e, left, scalar_copy)
+            interleave_w1(e, right, vector_copy)
+            multiply_layer1((0, 1, 2, 3), (0,))
             quantize_w(c)
-            quantize_x(4)
-            relu_w(p, True)
-            multiply_layer1((4,), (0,))
+            scale_x(5)
             quantize_w(e)
-            empty_layer1((1, 2, 3, 4), (0,))
+            relu_w(p, True)
+            empty_layer1((0, 1, 2, 3), (0,))
             widen_x((8, 9), scalar_copy)
+            quantize_x(4)
             multiply_w(p, left)
             interleave_w2_gpsimd(p, left)
             layer1((0, 1, 2, 3), (1,))
             scale_x(6, 7)
             widen_x((10, 11), scalar_copy)
+            relu_w(q, True)
             quantize_x(6)
             multiply_w(p, right)
             interleave_w2_gpsimd(p, right)
             turn_x(8, 9)
-            layer1((4,), (1,))
-            layer1((5,))
+            layer1((4, 5))
             scale_x(8, 9)
             widen_x((12, 13), scalar_copy)
-            relu_w(q, True)
+            quantize_w(p)
             quantize_x(8)
             multiply_w(q, left)
             interleave_w2_gpsimd(q, left)
@@ -341,7 +332,7 @@ def tile_sparse_connect_kernel(tc, x_bytes, x_scale, th1, sign1, th2, sign2, rel
             scale_x(10, 11)
             layer1((7,))
             widen_x((14, 15), scalar_copy)
-            quantize_w(p)
+            relu_w(s, True)
             quantize_x(10)
             multiply_w(q, right)
             interleave_w2_gpsimd(q, right)
@@ -349,12 +340,11 @@ def tile_sparse_connect_kernel(tc, x_bytes, x_scale, th1, sign1, th2, sign2, rel
             turn_x(12, 13)
             layer1((9,))
             turn_x(14, 15)
+            relu_w(r, False)
             scale_x(12, 13)
-            relu_w(s, True)
+            quantize_h(0)
             quantize_x(12)
             quantize_w(q)
-            relu_w(r, True)
-            quantize_h(0)
             layer1((10, 11))
             multiply_w(r)
             quantize_h(4)

@@ -45,6 +45,7 @@ def tile_sparse_connect_kernel(tc, x_bytes, x_scale, th1, sign1, th2, sign2, rel
         identity = keep.tile([P, P], F32, name="identity")
         make_identity(nc, identity[:])
         scale = keep.tile([P, 2, PACK], F32, name="scale", align_bytes=64)
+        scale_wide = keep.tile([P, 2, P, PACK], F32, name="scale_wide", align_bytes=64)
 
         theta, sign, grouped, w_codes, w_scales = {}, {}, {}, {}, {}
         x_in, x_wide, x_banks, x_grouped, x_codes, x_scales = {}, {}, {}, {}, {}, {}
@@ -106,12 +107,10 @@ def tile_sparse_connect_kernel(tc, x_bytes, x_scale, th1, sign1, th2, sign2, rel
                 in_=theta[piece][:, :, cols].rearrange("p j (m t) -> p m j t", t=PACK),
             )
 
-        def interleave_w2_vector(piece, cols):
-            nc.vector.tensor_copy(
-                out=grouped_tile(piece)[:, cols.start * PACK : cols.stop * PACK].rearrange(
-                    "p (c i j) -> p c j i", i=4, j=PACK
-                ),
-                in_=theta[piece][:, :, cols].rearrange("p j (c i) -> p c j i", i=4),
+        def interleave_w2(piece, copy):
+            copy(
+                out=grouped_tile(piece).rearrange("p (c i j) -> p c j i", i=4, j=PACK),
+                in_=theta[piece].rearrange("p j (c i) -> p c j i", i=4),
             )
 
         def interleave_w2_gpsimd(piece, cols):
@@ -162,7 +161,7 @@ def tile_sparse_connect_kernel(tc, x_bytes, x_scale, th1, sign1, th2, sign2, rel
                 nc.vector.tensor_tensor(
                     out=x_grouped[group][:, i - group].rearrange("p (g r u e) -> p g r u e", g=2, u=2, e=2),
                     in0=values.rearrange("p (u g r e) -> p g r u e", u=2, g=2, e=2),
-                    in1=scale[:].rearrange("p g (u e) -> p g u e", u=2).unsqueeze(2).to_broadcast([P, 2, P, 2, 2]),
+                    in1=scale_wide[:].rearrange("p g r (u e) -> p g r u e", u=2),
                     op=MULT,
                 )
                 free_banks.append(number)
@@ -276,32 +275,30 @@ def tile_sparse_connect_kernel(tc, x_bytes, x_scale, th1, sign1, th2, sign2, rel
             a, b, c, e = (1, 0, 0), (1, 0, 1), (1, 1, 0), (1, 1, 1)
             p, q, r, s = (2, 0, 0), (2, 0, 1), (2, 1, 0), (2, 1, 1)
             whole, left, right = slice(0, HALF), slice(0, PART), slice(PART, HALF)
+            vector_copy(out=scale_wide[:], in_=scale[:].unsqueeze(2).to_broadcast([P, 2, P, PACK]))
             widen_x((0, 1, 2, 3), scalar_copy)
             turn_x(0, 1, 2, 3)
             relu_w(a, False)
             scale_x(0, 1, 2)
             multiply_w(a)
-            widen_x((4, 5, 6), scalar_copy)
-            turn_x(4, 5)
+            widen_x((4, 5, 6, 7), scalar_copy)
+            turn_x(4, 5, 6, 7)
             interleave_w1(a, whole, scalar_copy)
-            widen_x((7,), scalar_copy)
-            scale_x(3)
             relu_w(b, True)
             quantize_x(0)
             multiply_w(b)
-            turn_x(6, 7)
             interleave_w1(b, whole, scalar_copy)
-            scale_x(4)
             relu_w(c, True)
-            quantize_w(a)
+            scale_x(3)
             multiply_w(c)
             interleave_w1(c, whole, scalar_copy)
+            quantize_w(a)
             relu_w(e, True)
             quantize_w(b)
             multiply_w(e)
+            interleave_w1(e, whole, scalar_copy)
+            scale_x(4)
             quantize_x(2)
-            interleave_w1(e, left, scalar_copy)
-            interleave_w1(e, right, vector_copy)
             multiply_layer1((0, 1, 2, 3), (0,))
             quantize_w(c)
             scale_x(5)
@@ -342,19 +339,19 @@ def tile_sparse_connect_kernel(tc, x_bytes, x_scale, th1, sign1, th2, sign2, rel
             turn_x(14, 15)
             relu_w(r, False)
             scale_x(12, 13)
-            quantize_h(0)
-            quantize_x(12)
             quantize_w(q)
+            quantize_x(12)
+            quantize_h(0)
             layer1((10, 11))
             multiply_w(r)
             quantize_h(4)
-            interleave_w2_vector(r, whole)
+            interleave_w2(r, vector_copy)
             layer1((12,))
             layer2(range(0, 4), 0)
             layer1((13,))
             multiply_w(s)
             quantize_h(8)
-            interleave_w2_vector(s, whole)
+            interleave_w2(s, vector_copy)
             quantize_w(r)
             quantize_w(s)
             quantize_h(12)

@@ -25,7 +25,12 @@ BANKS = 8
 
 LOADS = ((0, 1), (1, 1), (2, 2), (4, 4), (8, 4), (12, 4))
 X_GROUPS = ((0, 2), (2, 2), (4, 2), (6, 2), (8, 2), (10, 2), (12, 2), (14, 1), (15, 1))
-H_GROUPS = ((0, 4), (4, 4), (8, 4), (12, 2), (14, 1), (15, 1))
+H_GROUPS = ((0, 2), (2, 2), (4, 4), (8, 4), (12, 2), (14, 1), (15, 1))
+WIDE_BUFS = 8
+X_GROUPED_BUFS = 3
+X_CODES_BUFS = 6
+W_GROUPED_BUFS = 3
+RESULT_BUFS = 8
 
 
 def tile_sparse_connect_kernel(tc, x_bytes, x_scale, th1, sign1, th2, sign2, relu, out):
@@ -45,7 +50,6 @@ def tile_sparse_connect_kernel(tc, x_bytes, x_scale, th1, sign1, th2, sign2, rel
         identity = keep.tile([P, P], F32, name="identity")
         make_identity(nc, identity[:])
         scale = keep.tile([P, 2, PACK], F32, name="scale", align_bytes=64)
-        scale_wide = keep.tile([P, 2, P, PACK], F32, name="scale_wide", align_bytes=64)
 
         theta, sign, grouped, w_codes, w_scales = {}, {}, {}, {}, {}
         x_in, x_wide, x_banks, x_grouped, x_codes, x_scales = {}, {}, {}, {}, {}, {}
@@ -96,19 +100,19 @@ def tile_sparse_connect_kernel(tc, x_bytes, x_scale, th1, sign1, th2, sign2, rel
 
         def grouped_tile(piece):
             if piece not in grouped:
-                grouped[piece] = work.tile([P, HALF * PACK], BF16, name="w_grouped", bufs=3, align_bytes=64)
+                grouped[piece] = work.tile(
+                    [P, HALF * PACK], BF16, name="w_grouped", bufs=W_GROUPED_BUFS, align_bytes=64
+                )
             return grouped[piece][:]
 
-        def interleave_w1(piece, cols, copy):
-            copy(
-                out=grouped_tile(piece).rearrange("p (t m j) -> p m j t", t=PACK, j=PACK)[
-                    :, cols.start // PACK : cols.stop // PACK
-                ],
-                in_=theta[piece][:, :, cols].rearrange("p j (m t) -> p m j t", t=PACK),
+        def interleave_w1(piece):
+            nc.scalar.copy(
+                out=grouped_tile(piece).rearrange("p (t m j) -> p m j t", t=PACK, j=PACK),
+                in_=theta[piece].rearrange("p j (m t) -> p m j t", t=PACK),
             )
 
-        def interleave_w2(piece, copy):
-            copy(
+        def interleave_w2_vector(piece):
+            nc.vector.tensor_copy(
                 out=grouped_tile(piece).rearrange("p (c i j) -> p c j i", i=4, j=PACK),
                 in_=theta[piece].rearrange("p j (c i) -> p c j i", i=4),
             )
@@ -123,22 +127,18 @@ def tile_sparse_connect_kernel(tc, x_bytes, x_scale, th1, sign1, th2, sign2, rel
                 op1=ADD,
             )
 
-        def quantize_w(piece, cols=slice(0, HALF)):
-            if piece not in w_codes:
-                layer, half, g = piece
-                w_codes[piece] = keep.tile([P, HALF], U32, name=f"w_codes{layer}{half}{g}", align_bytes=64)
-                w_scales[piece] = keep.tile([P, HALF], U8, name=f"w_scales{layer}{half}{g}", align_bytes=64)
-            nc.vector.quantize_mx(
-                out=w_codes[piece][:, cols].bitcast(FP8X4),
-                scales=w_scales[piece][:, cols],
-                in_=grouped[piece][:, cols.start * PACK : cols.stop * PACK],
-            )
+        def quantize_w(piece):
+            layer, half, g = piece
+            codes = keep.tile([P, HALF], U32, name=f"w_codes{layer}{half}{g}", align_bytes=64)
+            scales = keep.tile([P, HALF], U8, name=f"w_scales{layer}{half}{g}", align_bytes=64)
+            nc.vector.quantize_mx(out=codes[:].bitcast(FP8X4), scales=scales[:], in_=grouped[piece][:])
+            w_codes[piece], w_scales[piece] = codes, scales
 
 
-        def widen_x(tiles, copy):
+        def widen_x(*tiles):
             for i in tiles:
-                x_wide[i] = work.tile([P, D], BF16, name="x_wide", bufs=8, align_bytes=64)
-                copy(out=x_wide[i][:], in_=x_in[i].bitcast(FP8))
+                x_wide[i] = work.tile([P, D], BF16, name="x_wide", bufs=WIDE_BUFS, align_bytes=64)
+                nc.scalar.copy(out=x_wide[i][:], in_=x_in[i].bitcast(FP8))
 
         def turn_x(*tiles):
             for i in tiles:
@@ -154,22 +154,22 @@ def tile_sparse_connect_kernel(tc, x_bytes, x_scale, th1, sign1, th2, sign2, rel
                 group = group_of(i, X_GROUPS)
                 if i == group:
                     x_grouped[group] = work.tile(
-                        [P, x_group_size[group], D], BF16, name="x_grouped", bufs=3, align_bytes=64
+                        [P, x_group_size[group], D], BF16, name="x_grouped", bufs=X_GROUPED_BUFS, align_bytes=64
                     )
                 bank, number = x_banks[i]
                 values = bank[:].rearrange("p u g r -> p (u g r)").bitcast(BF16)
                 nc.vector.tensor_tensor(
                     out=x_grouped[group][:, i - group].rearrange("p (g r u e) -> p g r u e", g=2, u=2, e=2),
                     in0=values.rearrange("p (u g r e) -> p g r u e", u=2, g=2, e=2),
-                    in1=scale_wide[:].rearrange("p g r (u e) -> p g r u e", u=2),
+                    in1=scale[:].rearrange("p g (u e) -> p g u e", u=2).unsqueeze(2).to_broadcast([P, 2, P, 2, 2]),
                     op=MULT,
                 )
                 free_banks.append(number)
 
         def quantize_x(group):
             count = x_group_size[group]
-            codes = work.tile([P, count, 2, P], U32, name="x_codes", bufs=6, align_bytes=64)
-            scales = work.tile([P, count, 2, P], U8, name="x_scales", bufs=6, align_bytes=64)
+            codes = work.tile([P, count, 2, P], U32, name="x_codes", bufs=X_CODES_BUFS, align_bytes=64)
+            scales = work.tile([P, count, 2, P], U8, name="x_scales", bufs=X_CODES_BUFS, align_bytes=64)
             nc.vector.quantize_mx(
                 out=codes[:].rearrange("p c g r -> p (c g r)").bitcast(FP8X4),
                 scales=scales[:].rearrange("p c g r -> p (c g r)"),
@@ -230,147 +230,129 @@ def tile_sparse_connect_kernel(tc, x_bytes, x_scale, th1, sign1, th2, sign2, rel
                 h_codes[group + c], h_scales[group + c] = codes[:, c], scales[:, c]
 
 
-        def layer2_columns(i, half, cols, on_vector):
-            width = cols.stop - cols.start
-            bank, number = take_bank([P, width], F32, "out_bank")
-            for g in (0, 1):
-                nc.tensor.matmul_mx(
-                    out=bank[:],
-                    lhsT=h_codes[i][:, g].bitcast(FP8X4),
-                    lhsT_scale=h_scales[i][:, g],
-                    rhs=w_codes[2, half, g][:, cols].bitcast(FP8X4),
-                    rhs_scale=w_scales[2, half, g][:, cols],
-                    start=(g == 0),
-                    stop=(g == 1),
-                )
-            result = work.tile([P, width], F32, name="result", bufs=8, align_bytes=64)
-            relu_on(result[:], bank[:], on_vector)
-            free_banks.append(number)
-            first, count = max(load for load in LOADS if load[0] <= i)
-            rows = out_rows[first * P : (first + count) * P, :].rearrange("(p c) n -> c p n", c=count)
-            nc.sync.dma_start(out=rows[i - first][:, half * HALF + cols.start : half * HALF + cols.stop], in_=result[:])
-
-        def layer2(tiles, half, cols=slice(0, HALF), on_vector=()):
+        def layer2(tiles, half, on_vector=()):
             for i in tiles:
-                layer2_columns(i, half, cols, i in on_vector)
+                bank, number = take_bank([P, HALF], F32, "out_bank")
+                for g in (0, 1):
+                    nc.tensor.matmul_mx(
+                        out=bank[:],
+                        lhsT=h_codes[i][:, g].bitcast(FP8X4),
+                        lhsT_scale=h_scales[i][:, g],
+                        rhs=w_codes[2, half, g][:].bitcast(FP8X4),
+                        rhs_scale=w_scales[2, half, g][:],
+                        start=(g == 0),
+                        stop=(g == 1),
+                    )
+                result = work.tile([P, HALF], F32, name="result", bufs=RESULT_BUFS, align_bytes=64)
+                relu_on(result[:], bank[:], i in on_vector)
+                free_banks.append(number)
+                first, count = max(load for load in LOADS if load[0] <= i)
+                rows = out_rows[first * P : (first + count) * P, :].rearrange("(p c) n -> c p n", c=count)
+                nc.sync.dma_start(out=rows[i - first][:, half * HALF : (half + 1) * HALF], in_=result[:])
 
-
-        scalar_copy, vector_copy = nc.scalar.copy, nc.vector.tensor_copy
 
         with tc.manual_schedule():
             nc.scalar.dma_start(out=scale[:], in_=x_scale.rearrange("a b (g p t) -> p (a b g) t", g=2, t=PACK))
-            load_x(*LOADS[0])
-            load_x(*LOADS[1])
-            load_x(*LOADS[2])
-            for half, g in ((0, 0), (0, 1), (1, 0), (1, 1)):
-                load_w1(theta_hbm, theta, half, g)
-                load_w1(sign_hbm, sign, half, g)
-                if (half, g) == (0, 0):
-                    load_x(*LOADS[3])
+            for load in LOADS[:3]:
+                load_x(*load)
+            for half in (0, 1):
+                for g in (0, 1):
+                    load_w1(theta_hbm, theta, half, g)
+                    load_w1(sign_hbm, sign, half, g)
+                    if (half, g) == (0, 0):
+                        load_x(*LOADS[3])
             for g in (0, 1):
                 load_w2(theta_hbm, theta, g)
                 load_w2(sign_hbm, sign, g)
                 load_x(*LOADS[4 + g])
 
-            a, b, c, e = (1, 0, 0), (1, 0, 1), (1, 1, 0), (1, 1, 1)
-            p, q, r, s = (2, 0, 0), (2, 0, 1), (2, 1, 0), (2, 1, 1)
-            whole, left, right = slice(0, HALF), slice(0, PART), slice(PART, HALF)
-            vector_copy(out=scale_wide[:], in_=scale[:].unsqueeze(2).to_broadcast([P, 2, P, PACK]))
-            widen_x((0, 1, 2, 3), scalar_copy)
+            widen_x(0, 1, 2, 3)
             turn_x(0, 1, 2, 3)
-            relu_w(a, False)
+            relu_w((1, 0, 0), on_vector=False)
             scale_x(0, 1, 2)
-            multiply_w(a)
-            widen_x((4, 5, 6, 7), scalar_copy)
+            multiply_w((1, 0, 0))
+            widen_x(4, 5, 6, 7)
             turn_x(4, 5, 6, 7)
-            interleave_w1(a, whole, scalar_copy)
-            relu_w(b, True)
+            interleave_w1((1, 0, 0))
+            relu_w((1, 0, 1), on_vector=True)
             quantize_x(0)
-            multiply_w(b)
-            interleave_w1(b, whole, scalar_copy)
-            relu_w(c, True)
+            multiply_w((1, 0, 1))
+            interleave_w1((1, 0, 1))
+            relu_w((1, 1, 0), on_vector=True)
             scale_x(3)
-            multiply_w(c)
-            interleave_w1(c, whole, scalar_copy)
-            quantize_w(a)
-            relu_w(e, True)
-            quantize_w(b)
-            multiply_w(e)
-            interleave_w1(e, whole, scalar_copy)
+            multiply_w((1, 1, 0))
+            interleave_w1((1, 1, 0))
+            quantize_w((1, 0, 0))
+            relu_w((1, 1, 1), on_vector=True)
+            quantize_w((1, 0, 1))
+            multiply_w((1, 1, 1))
+            interleave_w1((1, 1, 1))
             scale_x(4)
             quantize_x(2)
-            multiply_layer1((0, 1, 2, 3), (0,))
-            quantize_w(c)
+            multiply_layer1(range(4), (0,))
+            quantize_w((1, 1, 0))
             scale_x(5)
-            quantize_w(e)
-            relu_w(p, True)
-            empty_layer1((0, 1, 2, 3), (0,))
-            widen_x((8, 9), scalar_copy)
+            quantize_w((1, 1, 1))
+            relu_w((2, 0, 0), on_vector=True)
+            empty_layer1(range(4), (0,))
+            widen_x(8, 9)
+
+            left, right = slice(0, PART), slice(PART, HALF)
             quantize_x(4)
-            multiply_w(p, left)
-            interleave_w2_gpsimd(p, left)
-            layer1((0, 1, 2, 3), (1,))
+            multiply_w((2, 0, 0), left)
+            interleave_w2_gpsimd((2, 0, 0), left)
+            layer1(range(4), (1,))
             scale_x(6, 7)
-            widen_x((10, 11), scalar_copy)
-            relu_w(q, True)
-            quantize_x(6)
-            multiply_w(p, right)
-            interleave_w2_gpsimd(p, right)
-            turn_x(8, 9)
-            layer1((4, 5))
-            scale_x(8, 9)
-            widen_x((12, 13), scalar_copy)
-            quantize_w(p)
-            quantize_x(8)
-            multiply_w(q, left)
-            interleave_w2_gpsimd(q, left)
-            layer1((6,))
-            turn_x(10, 11)
-            scale_x(10, 11)
-            layer1((7,))
-            widen_x((14, 15), scalar_copy)
-            relu_w(s, True)
-            quantize_x(10)
-            multiply_w(q, right)
-            interleave_w2_gpsimd(q, right)
-            layer1((8,))
-            turn_x(12, 13)
-            layer1((9,))
-            turn_x(14, 15)
-            relu_w(r, False)
-            scale_x(12, 13)
-            quantize_w(q)
+            widen_x(10, 11)
+            relu_w((2, 0, 1), on_vector=True)
+            for pair, piece, cols in ((8, (2, 0, 0), right), (10, (2, 0, 1), left), (12, (2, 0, 1), right)):
+                quantize_x(pair - 2)
+                multiply_w(piece, cols)
+                interleave_w2_gpsimd(piece, cols)
+                layer1((pair - 4,))
+                turn_x(pair, pair + 1)
+                layer1((pair - 3,))
+                scale_x(pair, pair + 1)
+                if pair == 8:
+                    widen_x(12, 13)
+                    relu_w((2, 1, 1), on_vector=True)
+                elif pair == 10:
+                    widen_x(14, 15)
+                    quantize_w((2, 0, 0))
+                else:
+                    turn_x(14, 15)
+                    relu_w((2, 1, 0), on_vector=False)
+                    quantize_h(0)
             quantize_x(12)
-            quantize_h(0)
-            layer1((10, 11))
-            multiply_w(r)
+            quantize_w((2, 0, 1))
+            quantize_h(2)
+            layer1((10, 11, 12))
+
+            multiply_w((2, 1, 0))
             quantize_h(4)
-            interleave_w2(r, vector_copy)
-            layer1((12,))
+            interleave_w2_vector((2, 1, 0))
             layer2(range(0, 4), 0)
             layer1((13,))
-            multiply_w(s)
+            multiply_w((2, 1, 1))
             quantize_h(8)
-            interleave_w2(s, vector_copy)
-            quantize_w(r)
-            quantize_w(s)
+            interleave_w2_vector((2, 1, 1))
+            quantize_w((2, 1, 0))
+            quantize_w((2, 1, 1))
             quantize_h(12)
             layer2(range(4, 12), 0)
+
             scale_x(14, 15)
             quantize_x(14)
             quantize_x(15)
             odd = range(5, 16, 2)
-            layer2(range(0, 2), 1, whole, odd)
+            layer2(range(0, 2), 1)
             layer2(range(12, 14), 0)
-            layer2(range(2, 6), 1, whole, odd)
-            layer1((14,))
-            layer2(range(6, 8), 1, whole, odd)
-            quantize_h(14)
-            layer2(range(8, 10), 1, whole, odd)
-            layer1((15,))
-            layer2(range(10, 12), 1, whole, odd)
-            quantize_h(15)
-            layer2(range(12, 14), 1, whole, odd)
+            layer2(range(2, 6), 1, odd)
+            for last, first in ((14, 6), (15, 10)):
+                layer1((last,))
+                layer2(range(first, first + 2), 1, odd)
+                quantize_h(last)
+                layer2(range(first + 2, first + 4), 1, odd)
             for i in (14, 15):
                 layer2((i,), 0)
-                layer2((i,), 1, whole, (i,))
+                layer2((i,), 1, on_vector=(i,))

@@ -111,10 +111,14 @@ def tile_sparse_connect_kernel(tc, x_bytes, x_scale, th1, sign1, th2, sign2, rel
                 in_=theta[piece].rearrange("p j (m t) -> p m j t", t=PACK),
             )
 
-        def interleave_w2_vector(piece):
-            nc.vector.tensor_copy(
-                out=grouped_tile(piece).rearrange("p (c i j) -> p c j i", i=4, j=PACK),
-                in_=theta[piece].rearrange("p j (c i) -> p c j i", i=4),
+        def form_w2(piece):
+            nc.vector.scalar_tensor_tensor(
+                out=grouped_tile(piece).rearrange("p (c j) -> p c j", j=PACK),
+                in0=theta[piece].rearrange("p j c -> p c j"),
+                scalar=0.0,
+                in1=sign[piece].rearrange("p j c -> p c j"),
+                op0=MAX,
+                op1=MULT,
             )
 
         def interleave_w2_gpsimd(piece, cols):
@@ -315,27 +319,23 @@ def tile_sparse_connect_kernel(tc, x_bytes, x_scale, th1, sign1, th2, sign2, rel
                 scale_x(pair, pair + 1)
                 if pair == 8:
                     widen_x(12, 13)
-                    relu_w((2, 1, 1), on_vector=True)
+                    quantize_h(0)
                 elif pair == 10:
                     widen_x(14, 15)
                     quantize_w((2, 0, 0))
                 else:
                     turn_x(14, 15)
-                    relu_w((2, 1, 0), on_vector=False)
-                    quantize_h(0)
+                    quantize_h(2)
             quantize_x(12)
             quantize_w((2, 0, 1))
-            quantize_h(2)
             layer1((10, 11, 12))
 
-            multiply_w((2, 1, 0))
             quantize_h(4)
-            interleave_w2_vector((2, 1, 0))
+            form_w2((2, 1, 0))
             layer2(range(0, 4), 0)
             layer1((13,))
-            multiply_w((2, 1, 1))
             quantize_h(8)
-            interleave_w2_vector((2, 1, 1))
+            form_w2((2, 1, 1))
             quantize_w((2, 1, 0))
             quantize_w((2, 1, 1))
             quantize_h(12)

@@ -23,12 +23,13 @@ HALF = P * PACK
 PART = HALF // 2
 BANKS = 8
 
-LOADS = ((0, 1), (1, 1), (2, 2), (4, 4), (8, 4), (12, 4))
+LOADS = ((0, 1), (1, 1), (2, 2), (4, 2), (6, 2), (8, 2), (10, 2), (12, 4))
 X_GROUPS = ((0, 2), (2, 2), (4, 2), (6, 2), (8, 2), (10, 2), (12, 2), (14, 1), (15, 1))
-H_GROUPS = ((0, 2), (2, 2), (4, 4), (8, 4), (12, 2), (14, 1), (15, 1))
+H_GROUPS = ((0, 2), (2, 2), (4, 4), (8, 2), (10, 2), (12, 2), (14, 1), (15, 1))
 WIDE_BUFS = 8
 X_GROUPED_BUFS = 3
 X_CODES_BUFS = 6
+W_PRODUCT_BUFS = 2
 W_GROUPED_BUFS = 3
 RESULT_BUFS = 8
 
@@ -51,7 +52,7 @@ def tile_sparse_connect_kernel(tc, x_bytes, x_scale, th1, sign1, th2, sign2, rel
         make_identity(nc, identity[:])
         scale = keep.tile([P, 2, PACK], F32, name="scale", align_bytes=64)
 
-        theta, sign, grouped, w_codes, w_scales = {}, {}, {}, {}, {}
+        theta, sign, product, grouped, w_codes, w_scales = {}, {}, {}, {}, {}, {}
         x_in, x_wide, x_banks, x_grouped, x_codes, x_scales = {}, {}, {}, {}, {}, {}
         h_banks, h_grouped, h_codes, h_scales = {}, {}, {}, {}
         free_banks = list(range(BANKS))
@@ -71,16 +72,11 @@ def tile_sparse_connect_kernel(tc, x_bytes, x_scale, th1, sign1, th2, sign2, rel
                 nc.scalar.activation(out=out, in_=in_, func=RELU)
 
 
-        def load_w1(hbm, pieces, half, g):
-            t = keep.tile([P, PACK, HALF], BF16, name=f"w1_in{len(theta) + len(sign)}", align_bytes=64)
-            nc.sync.dma_start(out=t[:], in_=hbm[1][g][:, :, half * HALF : (half + 1) * HALF])
-            pieces[1, half, g] = t[:]
-
-        def load_w2(hbm, pieces, g):
-            t = keep.tile([P, PACK, N], BF16, name=f"w2_in{len(theta) + len(sign)}", align_bytes=64)
-            nc.sync.dma_start(out=t[:], in_=hbm[2][g])
-            for half in (0, 1):
-                pieces[2, half, g] = t[:, :, half * HALF : (half + 1) * HALF]
+        def load_w(layer, half, g, which=(0, 1)):
+            for hbm, pieces in (((theta_hbm, theta), (sign_hbm, sign))[n] for n in which):
+                t = keep.tile([P, PACK, HALF], BF16, name=f"w_in{len(theta) + len(sign)}", align_bytes=64)
+                nc.sync.dma_start(out=t[:], in_=hbm[layer][g][:, :, half * HALF : (half + 1) * HALF])
+                pieces[layer, half, g] = t[:]
 
         def load_x(first, count):
             t = keep.tile([P, count, D], U8, name=f"x_bytes{first}", align_bytes=64)
@@ -91,12 +87,22 @@ def tile_sparse_connect_kernel(tc, x_bytes, x_scale, th1, sign1, th2, sign2, rel
                 x_in[first + c] = t[:, c]
 
 
-        def relu_w(piece, on_vector):
-            relu_on(theta[piece], theta[piece], on_vector)
+        def relu_w(piece, engine="vector", rows=slice(0, PACK)):
+            th = theta[piece][:, rows]
+            if engine == "gpsimd":
+                nc.gpsimd.tensor_scalar(out=th, in0=th, scalar1=0.0, scalar2=1.0, op0=MAX, op1=MULT)
+            else:
+                relu_on(th, th, engine == "vector")
 
-        def multiply_w(piece, cols=slice(0, HALF)):
-            th = theta[piece][:, :, cols]
-            nc.vector.tensor_tensor(out=th, in0=th, in1=sign[piece][:, :, cols], op=MULT)
+        def multiply_w(piece, runs=slice(0, P)):
+            if piece not in product:
+                product[piece] = work.tile([P, P, PACK, PACK], BF16, name="w_product", bufs=W_PRODUCT_BUFS, align_bytes=64)
+            nc.vector.tensor_tensor(
+                out=product[piece][:, runs],
+                in0=theta[piece].rearrange("p j (m i) -> p m j i", i=PACK)[:, runs],
+                in1=sign[piece].rearrange("p j (m i) -> p m j i", i=PACK)[:, runs],
+                op=MULT,
+            )
 
         def grouped_tile(piece):
             if piece not in grouped:
@@ -105,31 +111,16 @@ def tile_sparse_connect_kernel(tc, x_bytes, x_scale, th1, sign1, th2, sign2, rel
                 )
             return grouped[piece][:]
 
-        def interleave_w1(piece):
-            nc.scalar.copy(
-                out=grouped_tile(piece).rearrange("p (t m j) -> p m j t", t=PACK, j=PACK),
-                in_=theta[piece].rearrange("p j (m t) -> p m j t", t=PACK),
-            )
-
-        def form_w2(piece):
-            nc.vector.scalar_tensor_tensor(
-                out=grouped_tile(piece).rearrange("p (c j) -> p c j", j=PACK),
-                in0=theta[piece].rearrange("p j c -> p c j"),
-                scalar=0.0,
-                in1=sign[piece].rearrange("p j c -> p c j"),
-                op0=MAX,
-                op1=MULT,
-            )
-
-        def interleave_w2_gpsimd(piece, cols):
-            nc.gpsimd.tensor_scalar(
-                out=grouped_tile(piece).rearrange("p (c j) -> p c j", j=PACK)[:, cols],
-                in0=theta[piece][:, :, cols].rearrange("p j c -> p c j"),
-                scalar1=1.0,
-                scalar2=0.0,
-                op0=MULT,
-                op1=ADD,
-            )
+        def interleave_w(piece, engine, runs=slice(0, P)):
+            order = "p (i m j) -> p m i j" if piece[0] == 1 else "p (m i j) -> p m i j"
+            dst = grouped_tile(piece).rearrange(order, i=PACK, j=PACK)[:, runs]
+            src = product[piece][:, runs].rearrange("p m j i -> p m i j")
+            if engine == "scalar":
+                nc.scalar.copy(out=dst, in_=src)
+            elif engine == "vector":
+                nc.vector.tensor_copy(out=dst, in_=src)
+            else:
+                nc.gpsimd.tensor_scalar(out=dst, in0=src, scalar1=1.0, scalar2=0.0, op0=MULT, op1=ADD)
 
         def quantize_w(piece):
             layer, half, g = piece
@@ -201,7 +192,7 @@ def tile_sparse_connect_kernel(tc, x_bytes, x_scale, th1, sign1, th2, sign2, rel
                             )
                     h_banks[i, half] = bank, number
 
-        def empty_layer1(tiles, halves):
+        def empty_layer1(tiles, halves, on_vector=False):
             for i in tiles:
                 group = group_of(i, H_GROUPS)
                 if group not in h_grouped:
@@ -210,9 +201,7 @@ def tile_sparse_connect_kernel(tc, x_bytes, x_scale, th1, sign1, th2, sign2, rel
                     )
                 for half in halves:
                     bank, number = h_banks[i, half]
-                    nc.scalar.activation(
-                        out=h_grouped[group][:, i - group, half], in_=bank[:].rearrange("p t n -> p n t"), func=RELU
-                    )
+                    relu_on(h_grouped[group][:, i - group, half], bank[:].rearrange("p t n -> p n t"), on_vector)
                     free_banks.append(number)
 
         def layer1(tiles, halves=(0, 1)):
@@ -254,105 +243,140 @@ def tile_sparse_connect_kernel(tc, x_bytes, x_scale, th1, sign1, th2, sign2, rel
                 rows = out_rows[first * P : (first + count) * P, :].rearrange("(p c) n -> c p n", c=count)
                 nc.sync.dma_start(out=rows[i - first][:, half * HALF : (half + 1) * HALF], in_=result[:])
 
-
         with tc.manual_schedule():
             nc.scalar.dma_start(out=scale[:], in_=x_scale.rearrange("a b (g p t) -> p (a b g) t", g=2, t=PACK))
-            for load in LOADS[:3]:
-                load_x(*load)
-            for half in (0, 1):
-                for g in (0, 1):
-                    load_w1(theta_hbm, theta, half, g)
-                    load_w1(sign_hbm, sign, half, g)
-                    if (half, g) == (0, 0):
-                        load_x(*LOADS[3])
-            for g in (0, 1):
-                load_w2(theta_hbm, theta, g)
-                load_w2(sign_hbm, sign, g)
-                load_x(*LOADS[4 + g])
+            load_x(*LOADS[0])
+            load_x(*LOADS[1])
+            load_w(1, 0, 0, (0,))
+            load_x(*LOADS[2])
+            load_x(*LOADS[3])
+            load_w(1, 0, 0, (1,))
+            load_x(*LOADS[4])
+            load_w(1, 0, 1, (0,))
+            load_x(*LOADS[5])
+            load_w(1, 0, 1, (1,))
+            load_w(1, 1, 0)
+            load_w(1, 1, 1)
+            load_x(*LOADS[6])
+            load_w(2, 0, 0)
+            load_w(2, 0, 1)
+            load_x(*LOADS[7])
+            load_w(2, 1, 0)
+            load_w(2, 1, 1)
 
-            widen_x(0, 1, 2, 3)
-            turn_x(0, 1, 2, 3)
-            relu_w((1, 0, 0), on_vector=False)
-            scale_x(0, 1, 2)
+            widen_x(0, 1)
+            turn_x(0, 1)
+            relu_w((1, 0, 0))
+            widen_x(2, 3, 4, 5)
+            turn_x(2, 3, 4, 5)
+            scale_x(0, 1)
             multiply_w((1, 0, 0))
-            widen_x(4, 5, 6, 7)
-            turn_x(4, 5, 6, 7)
-            interleave_w1((1, 0, 0))
-            relu_w((1, 0, 1), on_vector=True)
+            widen_x(6, 7)
+            turn_x(6, 7)
+            interleave_w((1, 0, 0), "scalar")
+            scale_x(2)
+            relu_w((1, 0, 1))
             quantize_x(0)
-            multiply_w((1, 0, 1))
-            interleave_w1((1, 0, 1))
-            relu_w((1, 1, 0), on_vector=True)
             scale_x(3)
-            multiply_w((1, 1, 0))
-            interleave_w1((1, 1, 0))
+            multiply_w((1, 0, 1))
+            widen_x(8, 9)
+            interleave_w((1, 0, 1), "scalar")
+            relu_w((1, 1, 0))
             quantize_w((1, 0, 0))
-            relu_w((1, 1, 1), on_vector=True)
+            multiply_w((1, 1, 0))
+            interleave_w((1, 1, 0), "scalar")
+            quantize_x(2)
+            relu_w((1, 1, 1))
             quantize_w((1, 0, 1))
             multiply_w((1, 1, 1))
-            interleave_w1((1, 1, 1))
-            scale_x(4)
-            quantize_x(2)
+            interleave_w((1, 1, 1), "scalar")
             multiply_layer1(range(4), (0,))
+            scale_x(4, 5)
             quantize_w((1, 1, 0))
-            scale_x(5)
-            quantize_w((1, 1, 1))
-            relu_w((2, 0, 0), on_vector=True)
-            empty_layer1(range(4), (0,))
-            widen_x(8, 9)
-
-            left, right = slice(0, PART), slice(PART, HALF)
             quantize_x(4)
-            multiply_w((2, 0, 0), left)
-            interleave_w2_gpsimd((2, 0, 0), left)
-            layer1(range(4), (1,))
-            scale_x(6, 7)
+            quantize_w((1, 1, 1))
+            relu_w((2, 0, 0))
+            multiply_layer1(range(4, 6), (0,))
+            empty_layer1(range(4), (0,))
+            multiply_layer1(range(2), (1,))
+            scale_x(6)
+            multiply_layer1(range(2, 4), (1,))
+            scale_x(7)
+            empty_layer1(range(4, 6), (0,))
+            turn_x(8, 9)
+            empty_layer1(range(2), (1,))
+            multiply_w((2, 0, 0))
+            quantize_x(6)
+            multiply_layer1(range(4, 6), (1,))
+            empty_layer1(range(2, 4), (1,))
             widen_x(10, 11)
-            relu_w((2, 0, 1), on_vector=True)
-            for pair, piece, cols in ((8, (2, 0, 0), right), (10, (2, 0, 1), left), (12, (2, 0, 1), right)):
-                quantize_x(pair - 2)
-                multiply_w(piece, cols)
-                interleave_w2_gpsimd(piece, cols)
-                layer1((pair - 4,))
-                turn_x(pair, pair + 1)
-                layer1((pair - 3,))
-                scale_x(pair, pair + 1)
-                if pair == 8:
-                    widen_x(12, 13)
-                    quantize_h(0)
-                elif pair == 10:
-                    widen_x(14, 15)
-                    quantize_w((2, 0, 0))
-                else:
-                    turn_x(14, 15)
-                    quantize_h(2)
-            quantize_x(12)
+            interleave_w((2, 0, 0), "gpsimd", slice(0, 96))
+            multiply_layer1((6,), (0, 1))
+            empty_layer1(range(4, 6), (1,))
+            scale_x(8)
+            turn_x(10, 11)
+            scale_x(9)
+            empty_layer1((6,), (0, 1))
+            widen_x(12, 13)
+            layer1((7,))
+            interleave_w((2, 0, 0), "vector", slice(96, P))
+            relu_w((2, 0, 1))
+            quantize_x(8)
+            multiply_w((2, 0, 1))
+            quantize_w((2, 0, 0))
+            interleave_w((2, 0, 1), "gpsimd", slice(0, 96))
+            scale_x(10)
+            layer1((8,))
+            turn_x(12, 13)
+            scale_x(11)
+            widen_x(14, 15)
+            layer1((9,))
+            interleave_w((2, 0, 1), "vector", slice(96, P))
+            quantize_x(10)
             quantize_w((2, 0, 1))
-            layer1((10, 11, 12))
-
+            quantize_h(0)
+            relu_w((2, 1, 0))
+            quantize_h(2)
+            multiply_w((2, 1, 0))
             quantize_h(4)
-            form_w2((2, 1, 0))
+            interleave_w((2, 1, 0), "gpsimd", slice(0, 96))
+            layer1((10, 11))
             layer2(range(0, 4), 0)
-            layer1((13,))
+            scale_x(12)
+            layer2(range(4, 6), 0)
+            scale_x(13)
+            turn_x(14, 15)
+            interleave_w((2, 1, 0), "vector", slice(96, P))
+            relu_w((2, 1, 1))
+            quantize_x(12)
             quantize_h(8)
-            form_w2((2, 1, 1))
+            multiply_w((2, 1, 1))
             quantize_w((2, 1, 0))
+            layer2(range(6, 8), 0)
+            layer1((12,))
+            layer2(range(8, 10), 0)
+            quantize_h(10)
+            interleave_w((2, 1, 1), "vector")
             quantize_w((2, 1, 1))
+            layer1((13,))
+            layer2(range(10, 12), 0)
+            scale_x(14)
             quantize_h(12)
-            layer2(range(4, 12), 0)
-
-            scale_x(14, 15)
+            scale_x(15)
             quantize_x(14)
+            layer2(range(0, 4), 1)
             quantize_x(15)
             odd = range(5, 16, 2)
-            layer2(range(0, 2), 1)
-            layer2(range(12, 14), 0)
-            layer2(range(2, 6), 1, odd)
-            for last, first in ((14, 6), (15, 10)):
-                layer1((last,))
-                layer2(range(first, first + 2), 1, odd)
-                quantize_h(last)
-                layer2(range(first + 2, first + 4), 1, odd)
-            for i in (14, 15):
-                layer2((i,), 0)
-                layer2((i,), 1, on_vector=(i,))
+            layer2(range(12, 14), 0, odd)
+            layer2(range(4, 6), 1, odd)
+            layer1((14,))
+            layer2(range(6, 8), 1, odd)
+            quantize_h(14)
+            layer2(range(8, 10), 1, odd)
+            layer1((15,))
+            layer2((14,), 0)
+            layer2((10,), 1, (10,))
+            quantize_h(15)
+            layer2(range(11, 15), 1, (12, 14))
+            layer2((15,), 0)
+            layer2((15,), 1, (15,))

@@ -25,12 +25,11 @@ BANKS = 8
 
 LOADS = ((0, 1), (1, 1), (2, 2), (4, 2), (6, 2), (8, 2), (10, 2), (12, 4))
 X_GROUPS = ((0, 2), (2, 2), (4, 2), (6, 2), (8, 2), (10, 2), (12, 2), (14, 1), (15, 1))
-H_GROUPS = ((0, 2), (2, 2), (4, 4), (8, 2), (10, 2), (12, 2), (14, 1), (15, 1))
-WIDE_BUFS = 8
+H_GROUPS = ((0, 4), (4, 4), (8, 4), (12, 2), (14, 1), (15, 1))
+WIDE_BUFS = 5
 X_GROUPED_BUFS = 3
 X_CODES_BUFS = 6
-W_PRODUCT_BUFS = 2
-W_GROUPED_BUFS = 3
+W_GROUPED_BUFS = 2
 RESULT_BUFS = 8
 
 
@@ -52,7 +51,8 @@ def tile_sparse_connect_kernel(tc, x_bytes, x_scale, th1, sign1, th2, sign2, rel
         make_identity(nc, identity[:])
         scale = keep.tile([P, 2, PACK], F32, name="scale", align_bytes=64)
 
-        theta, sign, product, grouped, w_codes, w_scales = {}, {}, {}, {}, {}, {}
+        theta, sign, grouped, w_codes, w_scales = {}, {}, {}, {}, {}
+        w2_in, w2_grouped = {}, {}
         x_in, x_wide, x_banks, x_grouped, x_codes, x_scales = {}, {}, {}, {}, {}, {}
         h_banks, h_grouped, h_codes, h_scales = {}, {}, {}, {}
         free_banks = list(range(BANKS))
@@ -72,11 +72,29 @@ def tile_sparse_connect_kernel(tc, x_bytes, x_scale, th1, sign1, th2, sign2, rel
                 nc.scalar.activation(out=out, in_=in_, func=RELU)
 
 
-        def load_w(layer, half, g, which=(0, 1)):
-            for hbm, pieces in (((theta_hbm, theta), (sign_hbm, sign))[n] for n in which):
-                t = keep.tile([P, PACK, HALF], BF16, name=f"w_in{len(theta) + len(sign)}", align_bytes=64)
-                nc.sync.dma_start(out=t[:], in_=hbm[layer][g][:, :, half * HALF : (half + 1) * HALF])
-                pieces[layer, half, g] = t[:]
+        def load_w(hbm, pieces, layer, half, g):
+            t = keep.tile([P, PACK, HALF], BF16, name=f"w_in{len(theta) + len(sign)}", align_bytes=64)
+            nc.sync.dma_start(out=t[:], in_=hbm[layer][g][:, :, half * HALF : (half + 1) * HALF])
+            pieces[layer, half, g] = t[:]
+
+        def load_theta(*piece):
+            load_w(theta_hbm, theta, *piece)
+
+        def load_sign(*piece):
+            load_w(sign_hbm, sign, *piece)
+
+        def load_w2(hbm, pieces, g):
+            t = keep.tile([P, PACK, N], BF16, name=f"w2_in{len(theta) + len(sign)}", align_bytes=64)
+            nc.sync.dma_start(out=t[:], in_=hbm[2][g])
+            for half in (0, 1):
+                pieces[2, half, g] = t[:, :, half * HALF : (half + 1) * HALF]
+
+        def load_w2_half(hbm, units, pieces, half):
+            t = keep.tile([P, 2, PACK, HALF], BF16, name=f"w2_in{half}{len(units)}", align_bytes=64)
+            for g in (0, 1):
+                nc.sync.dma_start(out=t[:, g], in_=hbm[2][g][:, :, half * HALF : (half + 1) * HALF])
+                pieces[2, half, g] = t[:, g]
+            units[hbm is sign_hbm, half] = t
 
         def load_x(first, count):
             t = keep.tile([P, count, D], U8, name=f"x_bytes{first}", align_bytes=64)
@@ -84,7 +102,7 @@ def tile_sparse_connect_kernel(tc, x_bytes, x_scale, th1, sign1, th2, sign2, rel
                 out=t[:], in_=x_rows[first * P : (first + count) * P, :].rearrange("(p c) d -> p c d", c=count)
             )
             for c in range(count):
-                x_in[first + c] = t[:, c]
+                x_in[first + c] = t[:].rearrange("p c d -> p (c d)")[:, c * D :]
 
 
         def relu_w(piece, engine="vector", rows=slice(0, PACK)):
@@ -94,15 +112,9 @@ def tile_sparse_connect_kernel(tc, x_bytes, x_scale, th1, sign1, th2, sign2, rel
             else:
                 relu_on(th, th, engine == "vector")
 
-        def multiply_w(piece, runs=slice(0, P)):
-            if piece not in product:
-                product[piece] = work.tile([P, P, PACK, PACK], BF16, name="w_product", bufs=W_PRODUCT_BUFS, align_bytes=64)
-            nc.vector.tensor_tensor(
-                out=product[piece][:, runs],
-                in0=theta[piece].rearrange("p j (m i) -> p m j i", i=PACK)[:, runs],
-                in1=sign[piece].rearrange("p j (m i) -> p m j i", i=PACK)[:, runs],
-                op=MULT,
-            )
+        def multiply_w(piece, cols=slice(0, HALF)):
+            th = theta[piece][:, :, cols]
+            nc.vector.tensor_tensor(out=th, in0=th, in1=sign[piece][:, :, cols], op=MULT)
 
         def grouped_tile(piece):
             if piece not in grouped:
@@ -111,16 +123,84 @@ def tile_sparse_connect_kernel(tc, x_bytes, x_scale, th1, sign1, th2, sign2, rel
                 )
             return grouped[piece][:]
 
-        def interleave_w(piece, engine, runs=slice(0, P)):
-            order = "p (i m j) -> p m i j" if piece[0] == 1 else "p (m i j) -> p m i j"
-            dst = grouped_tile(piece).rearrange(order, i=PACK, j=PACK)[:, runs]
-            src = product[piece][:, runs].rearrange("p m j i -> p m i j")
-            if engine == "scalar":
-                nc.scalar.copy(out=dst, in_=src)
-            elif engine == "vector":
-                nc.vector.tensor_copy(out=dst, in_=src)
-            else:
-                nc.gpsimd.tensor_scalar(out=dst, in0=src, scalar1=1.0, scalar2=0.0, op0=MULT, op1=ADD)
+        def interleave_w1(piece, runs=slice(0, P), on_vector=False):
+            move = nc.vector.tensor_copy if on_vector else nc.scalar.copy
+            move(
+                out=grouped_tile(piece).rearrange("p (t m j) -> p m j t", t=PACK, j=PACK)[:, runs],
+                in_=theta[piece].rearrange("p j (m t) -> p m j t", t=PACK)[:, runs],
+            )
+
+        def form_w1_gpsimd(piece, runs):
+            nc.gpsimd.tensor_tensor(
+                out=grouped_tile(piece).rearrange("p (t m j) -> p m t j", t=PACK, j=PACK)[:, runs],
+                in0=theta[piece].rearrange("p j (m t) -> p m t j", t=PACK)[:, runs],
+                in1=sign[piece].rearrange("p j (m t) -> p m t j", t=PACK)[:, runs],
+                op=MULT,
+            )
+
+        def interleave_w2_vector(piece, cols):
+            nc.vector.tensor_copy(
+                out=grouped_tile(piece).rearrange("p (c j) -> p c j", j=PACK)[:, cols],
+                in_=theta[piece][:, :, cols].rearrange("p j c -> p c j"),
+            )
+
+        def form_w2(piece):
+            grouped_w2(piece[1])
+            nc.vector.scalar_tensor_tensor(
+                out=grouped_tile(piece).rearrange("p (c j) -> p c j", j=PACK),
+                in0=theta[piece].rearrange("p j c -> p c j"),
+                scalar=0.0,
+                in1=sign[piece].rearrange("p j c -> p c j"),
+                op0=MAX,
+                op1=MULT,
+            )
+
+        def interleave_w2_gpsimd(piece, cols):
+            nc.gpsimd.tensor_scalar(
+                out=grouped_tile(piece).rearrange("p (c j) -> p c j", j=PACK)[:, cols],
+                in0=theta[piece][:, :, cols].rearrange("p j c -> p c j"),
+                scalar1=1.0,
+                scalar2=0.0,
+                op0=MULT,
+                op1=ADD,
+            )
+
+        def grouped_w2(half):
+            if half not in w2_grouped:
+                w2_grouped[half] = work.tile([P, 2, HALF, PACK], BF16, name="w2_grouped", align_bytes=64)
+                for g in (0, 1):
+                    grouped[2, half, g] = w2_grouped[half][:, g].rearrange("p c j -> p (c j)")
+            return w2_grouped[half]
+
+        def relu_w2(half):
+            th = w2_in[False, half][:].rearrange("p g j c -> p (g j c)")
+            relu_on(th, th, True)
+
+        def multiply_w2(half, cols):
+            th = w2_in[False, half][:].rearrange("p g j c -> p (g j) c")[:, :, cols]
+            sg = w2_in[True, half][:].rearrange("p g j c -> p (g j) c")[:, :, cols]
+            nc.vector.tensor_tensor(out=th, in0=th, in1=sg, op=MULT)
+
+        def interleave_w2(half, cols):
+            nc.gpsimd.tensor_scalar(
+                out=grouped_w2(half)[:, :, cols],
+                in0=w2_in[False, half][:, :, :, cols].rearrange("p g j c -> p g c j"),
+                scalar1=1.0,
+                scalar2=0.0,
+                op0=MULT,
+                op1=ADD,
+            )
+
+        def quantize_w2(half):
+            codes = keep.tile([P, 2, HALF], U32, name=f"w2_codes{half}", align_bytes=64)
+            scales = keep.tile([P, 2, HALF], U8, name=f"w2_scales{half}", align_bytes=64)
+            nc.vector.quantize_mx(
+                out=codes[:].rearrange("p g c -> p (g c)").bitcast(FP8X4),
+                scales=scales[:].rearrange("p g c -> p (g c)"),
+                in_=w2_grouped[half][:].rearrange("p g c j -> p (g c j)"),
+            )
+            for g in (0, 1):
+                w_codes[2, half, g], w_scales[2, half, g] = codes[:, g], scales[:, g]
 
         def quantize_w(piece):
             layer, half, g = piece
@@ -130,14 +210,15 @@ def tile_sparse_connect_kernel(tc, x_bytes, x_scale, th1, sign1, th2, sign2, rel
             w_codes[piece], w_scales[piece] = codes, scales
 
 
-        def widen_x(*tiles):
-            for i in tiles:
-                x_wide[i] = work.tile([P, D], BF16, name="x_wide", bufs=WIDE_BUFS, align_bytes=64)
-                nc.scalar.copy(out=x_wide[i][:], in_=x_in[i].bitcast(FP8))
+        def widen_x(first, count):
+            wide = work.tile([P, count * D], BF16, name="x_wide", bufs=WIDE_BUFS, align_bytes=64)
+            nc.scalar.copy(out=wide[:], in_=x_in[first][:, : count * D].bitcast(FP8))
+            for c in range(count):
+                x_wide[first + c] = wide[:, c * D : (c + 1) * D]
 
         def turn_x(*tiles):
             for i in tiles:
-                words = x_wide[i][:].bitcast(F32)
+                words = x_wide[i].bitcast(F32)
                 bank, number = take_bank([P, 2, 2, P], F32, "x_bank")
                 for g in (0, 1):
                     for u in (0, 1):
@@ -247,136 +328,124 @@ def tile_sparse_connect_kernel(tc, x_bytes, x_scale, th1, sign1, th2, sign2, rel
             nc.scalar.dma_start(out=scale[:], in_=x_scale.rearrange("a b (g p t) -> p (a b g) t", g=2, t=PACK))
             load_x(*LOADS[0])
             load_x(*LOADS[1])
-            load_w(1, 0, 0, (0,))
+            load_theta(1, 0, 0)
             load_x(*LOADS[2])
             load_x(*LOADS[3])
-            load_w(1, 0, 0, (1,))
+            load_sign(1, 0, 0)
             load_x(*LOADS[4])
-            load_w(1, 0, 1, (0,))
+            load_theta(1, 0, 1)
+            load_sign(1, 0, 1)
             load_x(*LOADS[5])
-            load_w(1, 0, 1, (1,))
-            load_w(1, 1, 0)
-            load_w(1, 1, 1)
+            for g in (0, 1):
+                load_theta(1, 1, g)
+                load_sign(1, 1, g)
+            load_w2_half(theta_hbm, w2_in, theta, 0)
             load_x(*LOADS[6])
-            load_w(2, 0, 0)
-            load_w(2, 0, 1)
+            load_w2_half(sign_hbm, w2_in, sign, 0)
             load_x(*LOADS[7])
-            load_w(2, 1, 0)
-            load_w(2, 1, 1)
+            load_w2_half(theta_hbm, w2_in, theta, 1)
+            load_w2_half(sign_hbm, w2_in, sign, 1)
 
             widen_x(0, 1)
+            widen_x(1, 1)
             turn_x(0, 1)
             relu_w((1, 0, 0))
-            widen_x(2, 3, 4, 5)
-            turn_x(2, 3, 4, 5)
+            widen_x(2, 2)
+            turn_x(2, 3)
+            widen_x(4, 2)
+            turn_x(4, 5)
             scale_x(0, 1)
             multiply_w((1, 0, 0))
-            widen_x(6, 7)
+            widen_x(6, 2)
             turn_x(6, 7)
-            interleave_w((1, 0, 0), "scalar")
+            interleave_w1((1, 0, 0))
             scale_x(2)
             relu_w((1, 0, 1))
             quantize_x(0)
-            scale_x(3)
             multiply_w((1, 0, 1))
-            widen_x(8, 9)
-            interleave_w((1, 0, 1), "scalar")
+            widen_x(8, 2)
+            interleave_w1((1, 0, 1))
+            scale_x(3)
             relu_w((1, 1, 0))
             quantize_w((1, 0, 0))
             multiply_w((1, 1, 0))
-            interleave_w((1, 1, 0), "scalar")
+            interleave_w1((1, 1, 0))
             quantize_x(2)
             relu_w((1, 1, 1))
             quantize_w((1, 0, 1))
             multiply_w((1, 1, 1))
-            interleave_w((1, 1, 1), "scalar")
+            interleave_w1((1, 1, 1))
             multiply_layer1(range(4), (0,))
             scale_x(4, 5)
             quantize_w((1, 1, 0))
             quantize_x(4)
             quantize_w((1, 1, 1))
-            relu_w((2, 0, 0))
             multiply_layer1(range(4, 6), (0,))
             empty_layer1(range(4), (0,))
+
+            parts = (slice(0, 152), slice(152, 332), slice(332, HALF))
             multiply_layer1(range(2), (1,))
             scale_x(6)
             multiply_layer1(range(2, 4), (1,))
             scale_x(7)
+            relu_w2(0)
             empty_layer1(range(4, 6), (0,))
             turn_x(8, 9)
             empty_layer1(range(2), (1,))
-            multiply_w((2, 0, 0))
             quantize_x(6)
+            multiply_w2(0, parts[0])
+            interleave_w2(0, parts[0])
             multiply_layer1(range(4, 6), (1,))
+            widen_x(10, 2)
             empty_layer1(range(2, 4), (1,))
-            widen_x(10, 11)
-            interleave_w((2, 0, 0), "gpsimd", slice(0, 96))
             multiply_layer1((6,), (0, 1))
             empty_layer1(range(4, 6), (1,))
             scale_x(8)
             turn_x(10, 11)
             scale_x(9)
             empty_layer1((6,), (0, 1))
-            widen_x(12, 13)
+            widen_x(12, 2)
             layer1((7,))
-            interleave_w((2, 0, 0), "vector", slice(96, P))
-            relu_w((2, 0, 1))
+            multiply_w2(0, parts[1])
             quantize_x(8)
-            multiply_w((2, 0, 1))
-            quantize_w((2, 0, 0))
-            interleave_w((2, 0, 1), "gpsimd", slice(0, 96))
+            interleave_w2(0, parts[1])
             scale_x(10)
             layer1((8,))
             turn_x(12, 13)
             scale_x(11)
-            widen_x(14, 15)
+            widen_x(14, 2)
             layer1((9,))
-            interleave_w((2, 0, 1), "vector", slice(96, P))
+            multiply_w2(0, parts[2])
             quantize_x(10)
-            quantize_w((2, 0, 1))
-            quantize_h(0)
-            relu_w((2, 1, 0))
-            quantize_h(2)
-            multiply_w((2, 1, 0))
-            quantize_h(4)
-            interleave_w((2, 1, 0), "gpsimd", slice(0, 96))
-            layer1((10, 11))
-            layer2(range(0, 4), 0)
+            interleave_w2(0, parts[2])
+            layer1((10,))
             scale_x(12)
-            layer2(range(4, 6), 0)
-            scale_x(13)
             turn_x(14, 15)
-            interleave_w((2, 1, 0), "vector", slice(96, P))
-            relu_w((2, 1, 1))
+            layer1((11,))
+            scale_x(13)
+            quantize_h(0)
             quantize_x(12)
-            quantize_h(8)
-            multiply_w((2, 1, 1))
-            quantize_w((2, 1, 0))
-            layer2(range(6, 8), 0)
+            quantize_w2(0)
             layer1((12,))
-            layer2(range(8, 10), 0)
-            quantize_h(10)
-            interleave_w((2, 1, 1), "vector")
-            quantize_w((2, 1, 1))
+            quantize_h(4)
+            form_w2((2, 1, 0))
+            layer2(range(0, 4), 0)
             layer1((13,))
-            layer2(range(10, 12), 0)
-            scale_x(14)
+            quantize_h(8)
+            form_w2((2, 1, 1))
             quantize_h(12)
-            scale_x(15)
+            quantize_w2(1)
+            layer2(range(4, 14), 0)
+            scale_x(14, 15)
             quantize_x(14)
-            layer2(range(0, 4), 1)
             quantize_x(15)
             odd = range(5, 16, 2)
-            layer2(range(12, 14), 0, odd)
-            layer2(range(4, 6), 1, odd)
-            layer1((14,))
-            layer2(range(6, 8), 1, odd)
-            quantize_h(14)
-            layer2(range(8, 10), 1, odd)
-            layer1((15,))
-            layer2((14,), 0)
-            layer2((10,), 1, (10,))
-            quantize_h(15)
-            layer2(range(11, 15), 1, (12, 14))
-            layer2((15,), 0)
-            layer2((15,), 1, (15,))
+            layer2(range(0, 6), 1, odd)
+            for last, first in ((14, 6), (15, 10)):
+                layer1((last,))
+                layer2(range(first, first + 2), 1, odd)
+                quantize_h(last)
+                layer2(range(first + 2, first + 4), 1, odd)
+            for i in (14, 15):
+                layer2((i,), 0)
+                layer2((i,), 1, on_vector=(i,))

@@ -13,10 +13,12 @@ U8 = mybir.dt.uint8
 FP8 = mybir.dt.float8_e4m3fn
 FP8X4 = mybir.dt.float8_e4m3fn_x4
 MAX = mybir.AluOpType.max
+MIN = mybir.AluOpType.min
 MULT = mybir.AluOpType.mult
 ADD = mybir.AluOpType.add
 RELU = mybir.ActivationFunctionType.Relu
 
+LARGEST = 3.4028234663852886e38
 P = 128
 PACK = 4
 HALF = P * PACK
@@ -26,9 +28,9 @@ BANKS = 8
 LOADS = ((0, 1), (1, 1), (2, 2), (4, 2), (6, 2), (8, 2), (10, 2), (12, 4))
 X_GROUPS = ((0, 2), (2, 2), (4, 2), (6, 2), (8, 2), (10, 2), (12, 2), (14, 1), (15, 1))
 H_GROUPS = ((0, 4), (4, 4), (8, 4), (12, 2), (14, 1), (15, 1))
-WIDE_BUFS = 5
+WIDE_BUFS = 4
 X_GROUPED_BUFS = 3
-X_CODES_BUFS = 6
+X_CODES_BUFS = 5
 W_GROUPED_BUFS = 2
 RESULT_BUFS = 8
 
@@ -52,7 +54,7 @@ def tile_sparse_connect_kernel(tc, x_bytes, x_scale, th1, sign1, th2, sign2, rel
         scale = keep.tile([P, 2, PACK], F32, name="scale", align_bytes=64)
 
         theta, sign, grouped, w_codes, w_scales = {}, {}, {}, {}, {}
-        w2_in, w2_grouped = {}, {}
+        w2_in, w2_grouped, first_raw, first_banks = {}, {}, {}, {}
         x_in, x_wide, x_banks, x_grouped, x_codes, x_scales = {}, {}, {}, {}, {}, {}
         h_banks, h_grouped, h_codes, h_scales = {}, {}, {}, {}
         free_banks = list(range(BANKS))
@@ -73,9 +75,11 @@ def tile_sparse_connect_kernel(tc, x_bytes, x_scale, th1, sign1, th2, sign2, rel
 
 
         def load_w(hbm, pieces, layer, half, g):
-            t = keep.tile([P, PACK, HALF], BF16, name=f"w_in{len(theta) + len(sign)}", align_bytes=64)
-            nc.sync.dma_start(out=t[:], in_=hbm[layer][g][:, :, half * HALF : (half + 1) * HALF])
-            pieces[layer, half, g] = t[:]
+            name = f"w_in{int(hbm is sign_hbm)}{half}{g}"
+            shape = [P, 2 * PACK, HALF] if name == "w_in111" else [P, PACK, HALF]
+            t = keep.tile(shape, BF16, name=name, align_bytes=64)
+            nc.sync.dma_start(out=t[:, :PACK], in_=hbm[layer][g][:, :, half * HALF : (half + 1) * HALF])
+            pieces[layer, half, g] = t[:, :PACK]
 
         def load_theta(*piece):
             load_w(theta_hbm, theta, *piece)
@@ -88,6 +92,13 @@ def tile_sparse_connect_kernel(tc, x_bytes, x_scale, th1, sign1, th2, sign2, rel
             nc.sync.dma_start(out=t[:], in_=hbm[2][g])
             for half in (0, 1):
                 pieces[2, half, g] = t[:, :, half * HALF : (half + 1) * HALF]
+
+        def load_w1_rows(hbm, pieces, g):
+            t = keep.tile([P, PACK, F], BF16, name=f"w1_rows{len(theta) + len(sign)}", align_bytes=64)
+            nc.sync.dma_start(out=t[:], in_=hbm[1][g])
+            for half in (0, 1):
+                pieces[1, half, g] = t[:, :, half * HALF : (half + 1) * HALF]
+            return t
 
         def load_w2_half(hbm, units, pieces, half):
             t = keep.tile([P, 2, PACK, HALF], BF16, name=f"w2_in{half}{len(units)}", align_bytes=64)
@@ -105,12 +116,22 @@ def tile_sparse_connect_kernel(tc, x_bytes, x_scale, th1, sign1, th2, sign2, rel
                 x_in[first + c] = t[:].rearrange("p c d -> p (c d)")[:, c * D :]
 
 
-        def relu_w(piece, engine="vector", rows=slice(0, PACK)):
-            th = theta[piece][:, rows]
+        def relu_w(piece, engine="vector", cols=slice(0, HALF)):
+            th = theta[piece][:, :, cols]
             if engine == "gpsimd":
-                nc.gpsimd.tensor_scalar(out=th, in0=th, scalar1=0.0, scalar2=1.0, op0=MAX, op1=MULT)
+                nc.gpsimd.tensor_scalar(out=th, in0=th, scalar1=LARGEST, scalar2=0.0, op0=MIN, op1=MAX)
             else:
                 relu_on(th, th, engine == "vector")
+
+        def interleave_w1_gpsimd(piece, runs):
+            nc.gpsimd.tensor_scalar(
+                out=grouped_tile(piece).rearrange("p (t m j) -> p m t j", t=PACK, j=PACK)[:, runs],
+                in0=theta[piece].rearrange("p j (m t) -> p m t j", t=PACK)[:, runs],
+                scalar1=1.0,
+                scalar2=0.0,
+                op0=MULT,
+                op1=ADD,
+            )
 
         def multiply_w(piece, cols=slice(0, HALF)):
             th = theta[piece][:, :, cols]
@@ -119,7 +140,7 @@ def tile_sparse_connect_kernel(tc, x_bytes, x_scale, th1, sign1, th2, sign2, rel
         def grouped_tile(piece):
             if piece not in grouped:
                 grouped[piece] = work.tile(
-                    [P, HALF * PACK], BF16, name="w_grouped", bufs=W_GROUPED_BUFS, align_bytes=64
+                    [P, HALF * PACK], BF16, name="w_grouped", tag=f"w_slot{piece[2]}", align_bytes=64
                 )
             return grouped[piece][:]
 
@@ -144,13 +165,13 @@ def tile_sparse_connect_kernel(tc, x_bytes, x_scale, th1, sign1, th2, sign2, rel
                 in_=theta[piece][:, :, cols].rearrange("p j c -> p c j"),
             )
 
-        def form_w2(piece):
+        def form_w2(piece, cols=slice(0, HALF)):
             grouped_w2(piece[1])
             nc.vector.scalar_tensor_tensor(
-                out=grouped_tile(piece).rearrange("p (c j) -> p c j", j=PACK),
-                in0=theta[piece].rearrange("p j c -> p c j"),
+                out=grouped_tile(piece).rearrange("p (c j) -> p c j", j=PACK)[:, cols],
+                in0=theta[piece].rearrange("p j c -> p c j")[:, cols],
                 scalar=0.0,
-                in1=sign[piece].rearrange("p j c -> p c j"),
+                in1=sign[piece].rearrange("p j c -> p c j")[:, cols],
                 op0=MAX,
                 op1=MULT,
             )
@@ -172,14 +193,34 @@ def tile_sparse_connect_kernel(tc, x_bytes, x_scale, th1, sign1, th2, sign2, rel
                     grouped[2, half, g] = w2_grouped[half][:, g].rearrange("p c j -> p (c j)")
             return w2_grouped[half]
 
-        def relu_w2(half):
-            th = w2_in[False, half][:].rearrange("p g j c -> p (g j c)")
-            relu_on(th, th, True)
+        def rows_w2(is_sign, half, cols):
+            return w2_in[is_sign, half][:].rearrange("p g j c -> p (g j) c")[:, :, cols]
 
-        def multiply_w2(half, cols):
-            th = w2_in[False, half][:].rearrange("p g j c -> p (g j) c")[:, :, cols]
-            sg = w2_in[True, half][:].rearrange("p g j c -> p (g j) c")[:, :, cols]
-            nc.vector.tensor_tensor(out=th, in0=th, in1=sg, op=MULT)
+        def relu_w2(half, cols):
+            relu_on(rows_w2(False, half, cols), rows_w2(False, half, cols), True)
+
+        def relu_gpsimd(out, in_):
+            nc.gpsimd.tensor_scalar(out=out, in0=in_, scalar1=LARGEST, scalar2=0.0, op0=MIN, op1=MAX)
+
+        def reuse(tag, rows, width):
+            t = keep.tile([P, rows, width], BF16, name="w_positive", tag=tag, align_bytes=64)
+            return t[:]
+
+        def relu_w2_gpsimd(half, cols):
+            width = cols.stop - cols.start
+            positive = work.tile(
+                [P, 2 * PACK, width], BF16, name="w_positive", tag="w_slot1", align_bytes=64
+            )
+            nc.gpsimd.tensor_scalar(
+                out=positive[:], in0=rows_w2(False, half, cols), scalar1=LARGEST, scalar2=0.0, op0=MIN, op1=MAX
+            )
+            return positive[:]
+
+        def multiply_w2(half, cols, positive=None):
+            th = rows_w2(False, half, cols)
+            nc.vector.tensor_tensor(
+                out=th, in0=th if positive is None else positive, in1=rows_w2(True, half, cols), op=MULT
+            )
 
         def interleave_w2(half, cols):
             nc.gpsimd.tensor_scalar(
@@ -215,6 +256,32 @@ def tile_sparse_connect_kernel(tc, x_bytes, x_scale, th1, sign1, th2, sign2, rel
             nc.scalar.copy(out=wide[:], in_=x_in[first][:, : count * D].bitcast(FP8))
             for c in range(count):
                 x_wide[first + c] = wide[:, c * D : (c + 1) * D]
+
+        def first_tile(g):
+            raw = keep.tile([P, HALF], U8, name=f"x_bytes_first{g}", align_bytes=64)
+            nc.sync.dma_start(out=raw[:], in_=x_rows[:P, g * HALF : (g + 1) * HALF])
+            first_raw[g] = raw
+
+        def turn_first(g):
+            wide = keep.tile([P, HALF], BF16, name=f"x_wide_first{g}", align_bytes=64)
+            nc.scalar.copy(out=wide[:], in_=first_raw[g][:].bitcast(FP8))
+            bank, number = take_bank([P, 2, P], F32, "x_bank")
+            for u in (0, 1):
+                nc.tensor.transpose(bank[:, u], wide[:].bitcast(F32)[:, u::2], identity[:])
+            first_banks[g] = bank, number
+
+        def scale_first(g):
+            if g == 0:
+                x_grouped[0] = work.tile([P, 2, D], BF16, name="x_grouped", bufs=X_GROUPED_BUFS, align_bytes=64)
+            bank, number = first_banks[g]
+            values = bank[:].rearrange("p u r -> p (u r)").bitcast(BF16)
+            nc.vector.tensor_tensor(
+                out=x_grouped[0][:, 0, g * HALF : (g + 1) * HALF].rearrange("p (r u e) -> p r u e", u=2, e=2),
+                in0=values.rearrange("p (u r e) -> p r u e", u=2, e=2),
+                in1=scale[:, g].rearrange("p (u e) -> p u e", u=2).unsqueeze(1).to_broadcast([P, P, 2, 2]),
+                op=MULT,
+            )
+            free_banks.append(number)
 
         def turn_x(*tiles):
             for i in tiles:
@@ -388,7 +455,7 @@ def tile_sparse_connect_kernel(tc, x_bytes, x_scale, th1, sign1, th2, sign2, rel
             scale_x(6)
             multiply_layer1(range(2, 4), (1,))
             scale_x(7)
-            relu_w2(0)
+            relu_w2(0, slice(0, HALF))
             empty_layer1(range(4, 6), (0,))
             turn_x(8, 9)
             empty_layer1(range(2), (1,))
@@ -441,11 +508,15 @@ def tile_sparse_connect_kernel(tc, x_bytes, x_scale, th1, sign1, th2, sign2, rel
             quantize_x(15)
             odd = range(5, 16, 2)
             layer2(range(0, 6), 1, odd)
-            for last, first in ((14, 6), (15, 10)):
-                layer1((last,))
-                layer2(range(first, first + 2), 1, odd)
-                quantize_h(last)
-                layer2(range(first + 2, first + 4), 1, odd)
-            for i in (14, 15):
-                layer2((i,), 0)
-                layer2((i,), 1, on_vector=(i,))
+            layer1((14,))
+            layer2(range(6, 8), 1, odd)
+            quantize_h(14)
+            layer2(range(8, 12), 1, odd)
+            multiply_layer1((15,), (0, 1))
+            empty_layer1((15,), (0,))
+            empty_layer1((15,), (1,), on_vector=True)
+            layer2((14,), 0)
+            quantize_h(15)
+            layer2((12, 13, 14), 1, (13,))
+            layer2((15,), 0, (15,))
+            layer2((15,), 1)

@@ -30,9 +30,9 @@ X_GROUPS = ((0, 2), (2, 2), (4, 2), (6, 2), (8, 2), (10, 2), (12, 2), (14, 1), (
 H_GROUPS = ((0, 4), (4, 4), (8, 4), (12, 2), (14, 1), (15, 1))
 WIDE_BUFS = 4
 X_GROUPED_BUFS = 3
-X_CODES_BUFS = 5
+X_CODES_BUFS = 6
 W_GROUPED_BUFS = 2
-RESULT_BUFS = 8
+RESULT_BUFS = 9
 
 
 def tile_sparse_connect_kernel(tc, x_bytes, x_scale, th1, sign1, th2, sign2, relu, out):
@@ -56,7 +56,7 @@ def tile_sparse_connect_kernel(tc, x_bytes, x_scale, th1, sign1, th2, sign2, rel
         theta, sign, grouped, w_codes, w_scales = {}, {}, {}, {}, {}
         w2_in, w2_grouped, first_raw, first_banks = {}, {}, {}, {}
         x_in, x_wide, x_banks, x_grouped, x_codes, x_scales = {}, {}, {}, {}, {}, {}
-        h_banks, h_grouped, h_codes, h_scales = {}, {}, {}, {}
+        h_banks, h_grouped, h_codes, h_scales, out_banks = {}, {}, {}, {}, {}
         free_banks = list(range(BANKS))
 
         def take_bank(shape, dtype, name):
@@ -123,16 +123,6 @@ def tile_sparse_connect_kernel(tc, x_bytes, x_scale, th1, sign1, th2, sign2, rel
             else:
                 relu_on(th, th, engine == "vector")
 
-        def interleave_w1_gpsimd(piece, runs):
-            nc.gpsimd.tensor_scalar(
-                out=grouped_tile(piece).rearrange("p (t m j) -> p m t j", t=PACK, j=PACK)[:, runs],
-                in0=theta[piece].rearrange("p j (m t) -> p m t j", t=PACK)[:, runs],
-                scalar1=1.0,
-                scalar2=0.0,
-                op0=MULT,
-                op1=ADD,
-            )
-
         def multiply_w(piece, cols=slice(0, HALF)):
             th = theta[piece][:, :, cols]
             nc.vector.tensor_tensor(out=th, in0=th, in1=sign[piece][:, :, cols], op=MULT)
@@ -188,7 +178,9 @@ def tile_sparse_connect_kernel(tc, x_bytes, x_scale, th1, sign1, th2, sign2, rel
 
         def grouped_w2(half):
             if half not in w2_grouped:
-                w2_grouped[half] = work.tile([P, 2, HALF, PACK], BF16, name="w2_grouped", align_bytes=64)
+                w2_grouped[half] = keep.tile(
+                    [P, 2, HALF, PACK], BF16, name="w2_grouped", tag=("w2_left", "w_in111")[half], align_bytes=64
+                )
                 for g in (0, 1):
                     grouped[2, half, g] = w2_grouped[half][:, g].rearrange("p c j -> p (c j)")
             return w2_grouped[half]
@@ -340,6 +332,23 @@ def tile_sparse_connect_kernel(tc, x_bytes, x_scale, th1, sign1, th2, sign2, rel
                             )
                     h_banks[i, half] = bank, number
 
+        def pass_layer1(tiles, half, g):
+            for i in tiles:
+                if g == 0:
+                    h_banks[i, half] = take_bank([P, PACK, P], F32, "h_bank")
+                bank, number = h_banks[i, half]
+                for t in range(PACK):
+                    cols = slice(t * P, (t + 1) * P)
+                    nc.tensor.matmul_mx(
+                        out=bank[:, t],
+                        lhsT=w_codes[1, half, g][:, cols].bitcast(FP8X4),
+                        lhsT_scale=w_scales[1, half, g][:, cols],
+                        rhs=x_codes[i][:, g].bitcast(FP8X4),
+                        rhs_scale=x_scales[i][:, g],
+                        start=(g == 0 and t == 0),
+                        stop=(g == 1 and t == PACK - 1),
+                    )
+
         def empty_layer1(tiles, halves, on_vector=False):
             for i in tiles:
                 group = group_of(i, H_GROUPS)
@@ -371,10 +380,22 @@ def tile_sparse_connect_kernel(tc, x_bytes, x_scale, th1, sign1, th2, sign2, rel
                 h_codes[group + c], h_scales[group + c] = codes[:, c], scales[:, c]
 
 
-        def layer2(tiles, half, on_vector=()):
+        def quantize_h_pass(i, g):
+            if g == 0:
+                h_codes[i] = keep.tile([P, 2, P], U32, name=f"h_codes{i}", align_bytes=64)[:]
+                h_scales[i] = keep.tile([P, 2, P], U8, name=f"h_scales{i}", align_bytes=64)[:]
+            nc.vector.quantize_mx(
+                out=h_codes[i][:, g].bitcast(FP8X4),
+                scales=h_scales[i][:, g],
+                in_=h_grouped[i][:, 0, g].rearrange("p n t -> p (n t)"),
+            )
+
+        def layer2(tiles, half, on_vector=(), passes=(0, 1)):
             for i in tiles:
-                bank, number = take_bank([P, HALF], F32, "out_bank")
-                for g in (0, 1):
+                if 0 in passes:
+                    out_banks[i, half] = take_bank([P, HALF], F32, "out_bank")
+                bank, number = out_banks[i, half]
+                for g in passes:
                     nc.tensor.matmul_mx(
                         out=bank[:],
                         lhsT=h_codes[i][:, g].bitcast(FP8X4),
@@ -384,6 +405,8 @@ def tile_sparse_connect_kernel(tc, x_bytes, x_scale, th1, sign1, th2, sign2, rel
                         start=(g == 0),
                         stop=(g == 1),
                     )
+                if 1 not in passes:
+                    continue
                 result = work.tile([P, HALF], F32, name="result", bufs=RESULT_BUFS, align_bytes=64)
                 relu_on(result[:], bank[:], i in on_vector)
                 free_banks.append(number)
@@ -496,13 +519,13 @@ def tile_sparse_connect_kernel(tc, x_bytes, x_scale, th1, sign1, th2, sign2, rel
             layer1((12,))
             quantize_h(4)
             form_w2((2, 1, 0))
-            layer2(range(0, 4), 0)
+            layer2(range(0, 7), 0)
             layer1((13,))
             quantize_h(8)
             form_w2((2, 1, 1))
             quantize_h(12)
             quantize_w2(1)
-            layer2(range(4, 14), 0)
+            layer2(range(7, 14), 0)
             scale_x(14, 15)
             quantize_x(14)
             quantize_x(15)
@@ -512,11 +535,14 @@ def tile_sparse_connect_kernel(tc, x_bytes, x_scale, th1, sign1, th2, sign2, rel
             layer2(range(6, 8), 1, odd)
             quantize_h(14)
             layer2(range(8, 12), 1, odd)
-            multiply_layer1((15,), (0, 1))
-            empty_layer1((15,), (0,))
-            empty_layer1((15,), (1,), on_vector=True)
             layer2((14,), 0)
-            quantize_h(15)
+            multiply_layer1((15,), (0, 1))
+            empty_layer1((15,), (0,), on_vector=True)
+            empty_layer1((15,), (1,))
+            quantize_h_pass(15, 0)
+            quantize_h_pass(15, 1)
             layer2((12, 13, 14), 1, (13,))
-            layer2((15,), 0, (15,))
-            layer2((15,), 1)
+            layer2((15,), 0, passes=(0,))
+            layer2((15,), 1, passes=(0,))
+            layer2((15,), 0, (15,), passes=(1,))
+            layer2((15,), 1, passes=(1,))

from contextlib import ExitStack

import concourse.mybir as mybir
from concourse.masks import make_identity

TOKENS, D, F, N = 2048, 1024, 1024, 1024
FLOPS = 2 * TOKENS * D * F + 2 * TOKENS * F * N

F32 = mybir.dt.float32
BF16 = mybir.dt.bfloat16
U32 = mybir.dt.uint32
U8 = mybir.dt.uint8
FP8 = mybir.dt.float8_e4m3fn
FP8X4 = mybir.dt.float8_e4m3fn_x4
MAX = mybir.AluOpType.max
MIN = mybir.AluOpType.min
MULT = mybir.AluOpType.mult
ADD = mybir.AluOpType.add
RELU = mybir.ActivationFunctionType.Relu

LARGEST = 3.4028234663852886e38
P = 128
PACK = 4
HALF = P * PACK
PART = HALF // 2
BANKS = 8

LOADS = ((0, 1), (1, 1), (2, 2), (4, 2), (6, 2), (8, 2), (10, 2), (12, 4))
X_GROUPS = ((0, 2), (2, 2), (4, 2), (6, 2), (8, 2), (10, 2), (12, 2), (14, 1), (15, 1))
H_GROUPS = ((0, 4), (4, 4), (8, 4), (12, 2), (14, 1), (15, 1))
WIDE_BUFS = 4
X_GROUPED_BUFS = 3
X_CODES_BUFS = 6
W_GROUPED_BUFS = 2
RESULT_BUFS = 9


def tile_sparse_connect_kernel(tc, x_bytes, x_scale, th1, sign1, th2, sign2, relu, out):
    assert relu == 1
    nc = tc.nc
    x_rows = x_bytes.flatten_outer_dims()
    out_rows = out.flatten_outer_dims()
    theta_hbm = {n: a.rearrange("(g p j) f -> g p j f", p=P, j=PACK) for n, a in ((1, th1), (2, th2))}
    sign_hbm = {n: a.rearrange("(g p j) f -> g p j f", p=P, j=PACK) for n, a in ((1, sign1), (2, sign2))}
    x_group_size, h_group_size = dict(X_GROUPS), dict(H_GROUPS)

    with ExitStack() as ctx:
        keep = ctx.enter_context(tc.tile_pool(name="keep", bufs=1))
        work = ctx.enter_context(tc.tile_pool(name="work", bufs=1))
        psum = ctx.enter_context(tc.psum_pool(name="psum", bufs=1))

        identity = keep.tile([P, P], F32, name="identity")
        make_identity(nc, identity[:])
        scale = keep.tile([P, 2, PACK], F32, name="scale", align_bytes=64)

        theta, sign, grouped, w_codes, w_scales = {}, {}, {}, {}, {}
        w2_in, w2_grouped, first_raw, first_banks = {}, {}, {}, {}
        x_in, x_wide, x_banks, x_grouped, x_codes, x_scales = {}, {}, {}, {}, {}, {}
        h_banks, h_grouped, h_codes, h_scales, out_banks = {}, {}, {}, {}, {}
        free_banks = list(range(BANKS))

        def take_bank(shape, dtype, name):
            number = free_banks[0]
            free_banks.remove(number)
            return psum.tile(shape, dtype, name=name, tag=f"bank{number}"), number

        def group_of(i, groups):
            return max(first for first, count in groups if first <= i)

        def relu_on(out, in_, on_vector):
            if on_vector:
                nc.vector.tensor_scalar(out=out, in0=in_, scalar1=0.0, scalar2=None, op0=MAX)
            else:
                nc.scalar.activation(out=out, in_=in_, func=RELU)


        def load_w(hbm, pieces, layer, half, g):
            name = f"w_in{int(hbm is sign_hbm)}{half}{g}"
            shape = [P, 2 * PACK, HALF] if name == "w_in111" else [P, PACK, HALF]
            t = keep.tile(shape, BF16, name=name, align_bytes=64)
            nc.sync.dma_start(out=t[:, :PACK], in_=hbm[layer][g][:, :, half * HALF : (half + 1) * HALF])
            pieces[layer, half, g] = t[:, :PACK]

        def load_theta(*piece):
            load_w(theta_hbm, theta, *piece)

        def load_sign(*piece):
            load_w(sign_hbm, sign, *piece)

        def load_w2(hbm, pieces, g):
            t = keep.tile([P, PACK, N], BF16, name=f"w2_in{len(theta) + len(sign)}", align_bytes=64)
            nc.sync.dma_start(out=t[:], in_=hbm[2][g])
            for half in (0, 1):
                pieces[2, half, g] = t[:, :, half * HALF : (half + 1) * HALF]

        def load_w1_rows(hbm, pieces, g):
            t = keep.tile([P, PACK, F], BF16, name=f"w1_rows{len(theta) + len(sign)}", align_bytes=64)
            nc.sync.dma_start(out=t[:], in_=hbm[1][g])
            for half in (0, 1):
                pieces[1, half, g] = t[:, :, half * HALF : (half + 1) * HALF]
            return t

        def load_w2_half(hbm, units, pieces, half):
            t = keep.tile([P, 2, PACK, HALF], BF16, name=f"w2_in{half}{len(units)}", align_bytes=64)
            for g in (0, 1):
                nc.sync.dma_start(out=t[:, g], in_=hbm[2][g][:, :, half * HALF : (half + 1) * HALF])
                pieces[2, half, g] = t[:, g]
            units[hbm is sign_hbm, half] = t

        def load_x(first, count):
            t = keep.tile([P, count, D], U8, name=f"x_bytes{first}", align_bytes=64)
            nc.sync.dma_start(
                out=t[:], in_=x_rows[first * P : (first + count) * P, :].rearrange("(p c) d -> p c d", c=count)
            )
            for c in range(count):
                x_in[first + c] = t[:].rearrange("p c d -> p (c d)")[:, c * D :]


        def relu_w(piece, engine="vector", cols=slice(0, HALF)):
            th = theta[piece][:, :, cols]
            if engine == "gpsimd":
                nc.gpsimd.tensor_scalar(out=th, in0=th, scalar1=LARGEST, scalar2=0.0, op0=MIN, op1=MAX)
            else:
                relu_on(th, th, engine == "vector")

        def multiply_w(piece, cols=slice(0, HALF)):
            th = theta[piece][:, :, cols]
            nc.vector.tensor_tensor(out=th, in0=th, in1=sign[piece][:, :, cols], op=MULT)

        def grouped_tile(piece):
            if piece not in grouped:
                grouped[piece] = work.tile(
                    [P, HALF * PACK], BF16, name="w_grouped", tag=f"w_slot{piece[2]}", align_bytes=64
                )
            return grouped[piece][:]

        def interleave_w1(piece, runs=slice(0, P), on_vector=False):
            move = nc.vector.tensor_copy if on_vector else nc.scalar.copy
            move(
                out=grouped_tile(piece).rearrange("p (t m j) -> p m j t", t=PACK, j=PACK)[:, runs],
                in_=theta[piece].rearrange("p j (m t) -> p m j t", t=PACK)[:, runs],
            )

        def form_w1_gpsimd(piece, runs):
            nc.gpsimd.tensor_tensor(
                out=grouped_tile(piece).rearrange("p (t m j) -> p m t j", t=PACK, j=PACK)[:, runs],
                in0=theta[piece].rearrange("p j (m t) -> p m t j", t=PACK)[:, runs],
                in1=sign[piece].rearrange("p j (m t) -> p m t j", t=PACK)[:, runs],
                op=MULT,
            )

        def interleave_w2_vector(piece, cols):
            nc.vector.tensor_copy(
                out=grouped_tile(piece).rearrange("p (c j) -> p c j", j=PACK)[:, cols],
                in_=theta[piece][:, :, cols].rearrange("p j c -> p c j"),
            )

        def form_w2(piece, cols=slice(0, HALF)):
            grouped_w2(piece[1])
            nc.vector.scalar_tensor_tensor(
                out=grouped_tile(piece).rearrange("p (c j) -> p c j", j=PACK)[:, cols],
                in0=theta[piece].rearrange("p j c -> p c j")[:, cols],
                scalar=0.0,
                in1=sign[piece].rearrange("p j c -> p c j")[:, cols],
                op0=MAX,
                op1=MULT,
            )

        def interleave_w2_gpsimd(piece, cols):
            nc.gpsimd.tensor_scalar(
                out=grouped_tile(piece).rearrange("p (c j) -> p c j", j=PACK)[:, cols],
                in0=theta[piece][:, :, cols].rearrange("p j c -> p c j"),
                scalar1=1.0,
                scalar2=0.0,
                op0=MULT,
                op1=ADD,
            )

        def grouped_w2(half):
            if half not in w2_grouped:
                w2_grouped[half] = keep.tile(
                    [P, 2, HALF, PACK], BF16, name="w2_grouped", tag=("w2_left", "w_in111")[half], align_bytes=64
                )
                for g in (0, 1):
                    grouped[2, half, g] = w2_grouped[half][:, g].rearrange("p c j -> p (c j)")
            return w2_grouped[half]

        def rows_w2(is_sign, half, cols):
            return w2_in[is_sign, half][:].rearrange("p g j c -> p (g j) c")[:, :, cols]

        def relu_w2(half, cols):
            relu_on(rows_w2(False, half, cols), rows_w2(False, half, cols), True)

        def relu_gpsimd(out, in_):
            nc.gpsimd.tensor_scalar(out=out, in0=in_, scalar1=LARGEST, scalar2=0.0, op0=MIN, op1=MAX)

        def reuse(tag, rows, width):
            t = keep.tile([P, rows, width], BF16, name="w_positive", tag=tag, align_bytes=64)
            return t[:]

        def relu_w2_gpsimd(half, cols):
            width = cols.stop - cols.start
            positive = work.tile(
                [P, 2 * PACK, width], BF16, name="w_positive", tag="w_slot1", align_bytes=64
            )
            nc.gpsimd.tensor_scalar(
                out=positive[:], in0=rows_w2(False, half, cols), scalar1=LARGEST, scalar2=0.0, op0=MIN, op1=MAX
            )
            return positive[:]

        def multiply_w2(half, cols, positive=None):
            th = rows_w2(False, half, cols)
            nc.vector.tensor_tensor(
                out=th, in0=th if positive is None else positive, in1=rows_w2(True, half, cols), op=MULT
            )

        def interleave_w2(half, cols):
            nc.gpsimd.tensor_scalar(
                out=grouped_w2(half)[:, :, cols],
                in0=w2_in[False, half][:, :, :, cols].rearrange("p g j c -> p g c j"),
                scalar1=1.0,
                scalar2=0.0,
                op0=MULT,
                op1=ADD,
            )

        def quantize_w2(half):
            codes = keep.tile([P, 2, HALF], U32, name=f"w2_codes{half}", align_bytes=64)
            scales = keep.tile([P, 2, HALF], U8, name=f"w2_scales{half}", align_bytes=64)
            nc.vector.quantize_mx(
                out=codes[:].rearrange("p g c -> p (g c)").bitcast(FP8X4),
                scales=scales[:].rearrange("p g c -> p (g c)"),
                in_=w2_grouped[half][:].rearrange("p g c j -> p (g c j)"),
            )
            for g in (0, 1):
                w_codes[2, half, g], w_scales[2, half, g] = codes[:, g], scales[:, g]

        def quantize_w(piece):
            layer, half, g = piece
            codes = keep.tile([P, HALF], U32, name=f"w_codes{layer}{half}{g}", align_bytes=64)
            scales = keep.tile([P, HALF], U8, name=f"w_scales{layer}{half}{g}", align_bytes=64)
            nc.vector.quantize_mx(out=codes[:].bitcast(FP8X4), scales=scales[:], in_=grouped[piece][:])
            w_codes[piece], w_scales[piece] = codes, scales


        def widen_x(first, count):
            wide = work.tile([P, count * D], BF16, name="x_wide", bufs=WIDE_BUFS, align_bytes=64)
            nc.scalar.copy(out=wide[:], in_=x_in[first][:, : count * D].bitcast(FP8))
            for c in range(count):
                x_wide[first + c] = wide[:, c * D : (c + 1) * D]

        def first_tile(g):
            raw = keep.tile([P, HALF], U8, name=f"x_bytes_first{g}", align_bytes=64)
            nc.sync.dma_start(out=raw[:], in_=x_rows[:P, g * HALF : (g + 1) * HALF])
            first_raw[g] = raw

        def turn_first(g):
            wide = keep.tile([P, HALF], BF16, name=f"x_wide_first{g}", align_bytes=64)
            nc.scalar.copy(out=wide[:], in_=first_raw[g][:].bitcast(FP8))
            bank, number = take_bank([P, 2, P], F32, "x_bank")
            for u in (0, 1):
                nc.tensor.transpose(bank[:, u], wide[:].bitcast(F32)[:, u::2], identity[:])
            first_banks[g] = bank, number

        def scale_first(g):
            if g == 0:
                x_grouped[0] = work.tile([P, 2, D], BF16, name="x_grouped", bufs=X_GROUPED_BUFS, align_bytes=64)
            bank, number = first_banks[g]
            values = bank[:].rearrange("p u r -> p (u r)").bitcast(BF16)
            nc.vector.tensor_tensor(
                out=x_grouped[0][:, 0, g * HALF : (g + 1) * HALF].rearrange("p (r u e) -> p r u e", u=2, e=2),
                in0=values.rearrange("p (u r e) -> p r u e", u=2, e=2),
                in1=scale[:, g].rearrange("p (u e) -> p u e", u=2).unsqueeze(1).to_broadcast([P, P, 2, 2]),
                op=MULT,
            )
            free_banks.append(number)

        def turn_x(*tiles):
            for i in tiles:
                words = x_wide[i].bitcast(F32)
                bank, number = take_bank([P, 2, 2, P], F32, "x_bank")
                for g in (0, 1):
                    for u in (0, 1):
                        nc.tensor.transpose(bank[:, u, g], words[:, 256 * g + u : 256 * (g + 1) : 2], identity[:])
                x_banks[i] = bank, number

        def scale_x(*tiles):
            for i in tiles:
                group = group_of(i, X_GROUPS)
                if i == group:
                    x_grouped[group] = work.tile(
                        [P, x_group_size[group], D], BF16, name="x_grouped", bufs=X_GROUPED_BUFS, align_bytes=64
                    )
                bank, number = x_banks[i]
                values = bank[:].rearrange("p u g r -> p (u g r)").bitcast(BF16)
                nc.vector.tensor_tensor(
                    out=x_grouped[group][:, i - group].rearrange("p (g r u e) -> p g r u e", g=2, u=2, e=2),
                    in0=values.rearrange("p (u g r e) -> p g r u e", u=2, g=2, e=2),
                    in1=scale[:].rearrange("p g (u e) -> p g u e", u=2).unsqueeze(2).to_broadcast([P, 2, P, 2, 2]),
                    op=MULT,
                )
                free_banks.append(number)

        def quantize_x(group):
            count = x_group_size[group]
            codes = work.tile([P, count, 2, P], U32, name="x_codes", bufs=X_CODES_BUFS, align_bytes=64)
            scales = work.tile([P, count, 2, P], U8, name="x_scales", bufs=X_CODES_BUFS, align_bytes=64)
            nc.vector.quantize_mx(
                out=codes[:].rearrange("p c g r -> p (c g r)").bitcast(FP8X4),
                scales=scales[:].rearrange("p c g r -> p (c g r)"),
                in_=x_grouped[group][:].rearrange("p c d -> p (c d)"),
            )
            for c in range(count):
                x_codes[group + c], x_scales[group + c] = codes[:, c], scales[:, c]


        def multiply_layer1(tiles, halves):
            for i in tiles:
                for half in halves:
                    bank, number = take_bank([P, PACK, P], F32, "h_bank")
                    for t in range(PACK):
                        cols = slice(t * P, (t + 1) * P)
                        for g in (0, 1):
                            nc.tensor.matmul_mx(
                                out=bank[:, t],
                                lhsT=w_codes[1, half, g][:, cols].bitcast(FP8X4),
                                lhsT_scale=w_scales[1, half, g][:, cols],
                                rhs=x_codes[i][:, g].bitcast(FP8X4),
                                rhs_scale=x_scales[i][:, g],
                                start=(g == 0),
                                stop=(g == 1),
                            )
                    h_banks[i, half] = bank, number

        def pass_layer1(tiles, half, g):
            for i in tiles:
                if g == 0:
                    h_banks[i, half] = take_bank([P, PACK, P], F32, "h_bank")
                bank, number = h_banks[i, half]
                for t in range(PACK):
                    cols = slice(t * P, (t + 1) * P)
                    nc.tensor.matmul_mx(
                        out=bank[:, t],
                        lhsT=w_codes[1, half, g][:, cols].bitcast(FP8X4),
                        lhsT_scale=w_scales[1, half, g][:, cols],
                        rhs=x_codes[i][:, g].bitcast(FP8X4),
                        rhs_scale=x_scales[i][:, g],
                        start=(g == 0 and t == 0),
                        stop=(g == 1 and t == PACK - 1),
                    )

        def empty_layer1(tiles, halves, on_vector=False):
            for i in tiles:
                group = group_of(i, H_GROUPS)
                if group not in h_grouped:
                    h_grouped[group] = keep.tile(
                        [P, h_group_size[group], 2, P, PACK], BF16, name=f"h_grouped{group}", align_bytes=64
                    )
                for half in halves:
                    bank, number = h_banks[i, half]
                    relu_on(h_grouped[group][:, i - group, half], bank[:].rearrange("p t n -> p n t"), on_vector)
                    free_banks.append(number)

        def layer1(tiles, halves=(0, 1)):
            for i in tiles:
                for half in halves:
                    multiply_layer1((i,), (half,))
                    empty_layer1((i,), (half,))

        def quantize_h(group):
            count = h_group_size[group]
            codes = keep.tile([P, count, 2, P], U32, name=f"h_codes{group}", align_bytes=64)
            scales = keep.tile([P, count, 2, P], U8, name=f"h_scales{group}", align_bytes=64)
            nc.vector.quantize_mx(
                out=codes[:].rearrange("p c g n -> p (c g n)").bitcast(FP8X4),
                scales=scales[:].rearrange("p c g n -> p (c g n)"),
                in_=h_grouped[group][:].rearrange("p c g n t -> p (c g n t)"),
            )
            for c in range(count):
                h_codes[group + c], h_scales[group + c] = codes[:, c], scales[:, c]


        def quantize_h_pass(i, g):
            if g == 0:
                h_codes[i] = keep.tile([P, 2, P], U32, name=f"h_codes{i}", align_bytes=64)[:]
                h_scales[i] = keep.tile([P, 2, P], U8, name=f"h_scales{i}", align_bytes=64)[:]
            nc.vector.quantize_mx(
                out=h_codes[i][:, g].bitcast(FP8X4),
                scales=h_scales[i][:, g],
                in_=h_grouped[i][:, 0, g].rearrange("p n t -> p (n t)"),
            )

        def layer2(tiles, half, on_vector=(), passes=(0, 1)):
            for i in tiles:
                if 0 in passes:
                    out_banks[i, half] = take_bank([P, HALF], F32, "out_bank")
                bank, number = out_banks[i, half]
                for g in passes:
                    nc.tensor.matmul_mx(
                        out=bank[:],
                        lhsT=h_codes[i][:, g].bitcast(FP8X4),
                        lhsT_scale=h_scales[i][:, g],
                        rhs=w_codes[2, half, g][:].bitcast(FP8X4),
                        rhs_scale=w_scales[2, half, g][:],
                        start=(g == 0),
                        stop=(g == 1),
                    )
                if 1 not in passes:
                    continue
                result = work.tile([P, HALF], F32, name="result", bufs=RESULT_BUFS, align_bytes=64)
                relu_on(result[:], bank[:], i in on_vector)
                free_banks.append(number)
                first, count = max(load for load in LOADS if load[0] <= i)
                rows = out_rows[first * P : (first + count) * P, :].rearrange("(p c) n -> c p n", c=count)
                nc.sync.dma_start(out=rows[i - first][:, half * HALF : (half + 1) * HALF], in_=result[:])

        with tc.manual_schedule():
            nc.scalar.dma_start(out=scale[:], in_=x_scale.rearrange("a b (g p t) -> p (a b g) t", g=2, t=PACK))
            load_x(*LOADS[0])
            load_x(*LOADS[1])
            load_theta(1, 0, 0)
            load_x(*LOADS[2])
            load_x(*LOADS[3])
            load_sign(1, 0, 0)
            load_x(*LOADS[4])
            load_theta(1, 0, 1)
            load_sign(1, 0, 1)
            load_x(*LOADS[5])
            for g in (0, 1):
                load_theta(1, 1, g)
                load_sign(1, 1, g)
            load_w2_half(theta_hbm, w2_in, theta, 0)
            load_x(*LOADS[6])
            load_w2_half(sign_hbm, w2_in, sign, 0)
            load_x(*LOADS[7])
            load_w2_half(theta_hbm, w2_in, theta, 1)
            load_w2_half(sign_hbm, w2_in, sign, 1)

            widen_x(0, 1)
            widen_x(1, 1)
            turn_x(0, 1)
            relu_w((1, 0, 0))
            widen_x(2, 2)
            turn_x(2, 3)
            widen_x(4, 2)
            turn_x(4, 5)
            scale_x(0, 1)
            multiply_w((1, 0, 0))
            widen_x(6, 2)
            turn_x(6, 7)
            interleave_w1((1, 0, 0))
            scale_x(2)
            relu_w((1, 0, 1))
            quantize_x(0)
            multiply_w((1, 0, 1))
            widen_x(8, 2)
            interleave_w1((1, 0, 1))
            scale_x(3)
            relu_w((1, 1, 0))
            quantize_w((1, 0, 0))
            multiply_w((1, 1, 0))
            interleave_w1((1, 1, 0))
            quantize_x(2)
            relu_w((1, 1, 1))
            quantize_w((1, 0, 1))
            multiply_w((1, 1, 1))
            interleave_w1((1, 1, 1))
            multiply_layer1(range(4), (0,))
            scale_x(4, 5)
            quantize_w((1, 1, 0))
            quantize_x(4)
            quantize_w((1, 1, 1))
            multiply_layer1(range(4, 6), (0,))
            empty_layer1(range(4), (0,))

            parts = (slice(0, 152), slice(152, 332), slice(332, HALF))
            multiply_layer1(range(2), (1,))
            scale_x(6)
            multiply_layer1(range(2, 4), (1,))
            scale_x(7)
            relu_w2(0, slice(0, HALF))
            empty_layer1(range(4, 6), (0,))
            turn_x(8, 9)
            empty_layer1(range(2), (1,))
            quantize_x(6)
            multiply_w2(0, parts[0])
            interleave_w2(0, parts[0])
            multiply_layer1(range(4, 6), (1,))
            widen_x(10, 2)
            empty_layer1(range(2, 4), (1,))
            multiply_layer1((6,), (0, 1))
            empty_layer1(range(4, 6), (1,))
            scale_x(8)
            turn_x(10, 11)
            scale_x(9)
            empty_layer1((6,), (0, 1))
            widen_x(12, 2)
            layer1((7,))
            multiply_w2(0, parts[1])
            quantize_x(8)
            interleave_w2(0, parts[1])
            scale_x(10)
            layer1((8,))
            turn_x(12, 13)
            scale_x(11)
            widen_x(14, 2)
            layer1((9,))
            multiply_w2(0, parts[2])
            quantize_x(10)
            interleave_w2(0, parts[2])
            layer1((10,))
            scale_x(12)
            turn_x(14, 15)
            layer1((11,))
            scale_x(13)
            quantize_h(0)
            quantize_x(12)
            quantize_w2(0)
            layer1((12,))
            quantize_h(4)
            form_w2((2, 1, 0))
            layer2(range(0, 7), 0)
            layer1((13,))
            quantize_h(8)
            form_w2((2, 1, 1))
            quantize_h(12)
            quantize_w2(1)
            layer2(range(7, 14), 0)
            scale_x(14, 15)
            quantize_x(14)
            quantize_x(15)
            odd = range(5, 16, 2)
            layer2(range(0, 6), 1, odd)
            layer1((14,))
            layer2(range(6, 8), 1, odd)
            quantize_h(14)
            layer2(range(8, 12), 1, odd)
            layer2((14,), 0)
            multiply_layer1((15,), (0, 1))
            empty_layer1((15,), (0,), on_vector=True)
            empty_layer1((15,), (1,))
            quantize_h_pass(15, 0)
            quantize_h_pass(15, 1)
            layer2((12, 13, 14), 1, (13,))
            layer2((15,), 0, passes=(0,))
            layer2((15,), 1, passes=(0,))
            layer2((15,), 0, (15,), passes=(1,))
            layer2((15,), 1, passes=(1,))
